import numpy as np
import ml_dtypes


def mxq(x, axis, fmt="e4m3"):
    dtype, down = {"e4m3": (ml_dtypes.float8_e4m3fn, 7), "e5m2": (ml_dtypes.float8_e5m2, 14)}[fmt]
    v = np.moveaxis(np.asarray(x, np.float32).astype(ml_dtypes.bfloat16).astype(np.float64), axis, -1)
    blocks = v.reshape(v.shape[:-1] + (-1, 32))
    amax = np.abs(blocks).max(-1, keepdims=True)
    byte = np.maximum(np.where(amax > 0, np.frexp(amax)[1] - 1 + 127, 0) - down, 1)
    scale = np.exp2(byte - 127.0)
    codes = (blocks / scale).astype(np.float32).astype(dtype).astype(np.float64)
    return np.moveaxis((codes * scale).reshape(v.shape), -1, axis)


WIDE = False


def mx_kscale(k):
    if not WIDE:
        return np.ones(k)
    levels = np.array([10, -10, 5, -5, 0])
    if k % 512:
        return np.exp2(np.random.permutation(np.resize(levels, k // 32))).repeat(32)
    a = np.empty((k // 512, 16))
    for p in range(k // 512):
        a[p, :8] = np.random.permutation(np.resize(levels, 8))
        for g in range(8):
            far = levels[np.abs(levels - a[p, g]) >= 10]
            a[p, g + 8] = far[np.random.randint(len(far))]
    return np.exp2(a.ravel()).repeat(32)


BF16 = ml_dtypes.bfloat16


def bf(x):
    return np.asarray(x, np.float32).astype(BF16)


def f64(x):
    return np.asarray(x).astype(np.float64)


NQ, NK, QS, KS, F, DEG = 1024, 1024, 512, 512, 512, 32
EPS = 1e-5
SLOPE = 0.01


def leaky(v):
    return np.where(v >= 0, v, SLOPE * v)


def draw0():
    s, t = mx_kscale(QS), mx_kscale(F)
    return {"x": bf(np.random.standard_normal((NQ, QS)) * s),
            "w1": bf(np.random.standard_normal((QS, F)) / np.sqrt(QS) / s[:, None] * t),
            "b1": bf(np.random.standard_normal(F) * 0.5 * t),
            "w2": bf(np.random.standard_normal((F, F)) / np.sqrt(F) / t[:, None]),
            "b2": bf(np.random.standard_normal(F) * 0.5),
            "gamma": bf(1.0 + 0.1 * np.random.standard_normal(F)),
            "beta": bf(0.1 * np.random.standard_normal(F))}


def core(x, w1, b1, w2, b2, gamma, beta):
    h = leaky((mxq(f64(x), 1, "e4m3") @ mxq(f64(w1), 0, "e4m3")) + f64(b1))
    h = leaky((mxq(h, 1, "e4m3") @ mxq(f64(w2), 0, "e4m3")) + f64(b2))
    mean = h.mean(axis=0)
    var = h.var(axis=0)
    return f64(gamma) * (h - mean) / np.sqrt(var + EPS) + f64(beta)


def e4m3fn_bytes(y):
    return np.clip(np.asarray(y, np.float64), -448.0, 448.0).astype(np.float32).astype(ml_dtypes.float8_e4m3fn).view(np.uint8)


def e4m3fn_values(b):
    return np.asarray(b, np.uint8).view(ml_dtypes.float8_e4m3fn).astype(np.float64)


def setup_inputs():
    d = draw0()
    x0 = np.asarray(d['x']).astype(np.float64)
    s = (np.max(np.abs(x0), axis=(0,), keepdims=True) / 448.0).astype(np.float32)
    out = {}
    for k, v in d.items():
        if k == 'x':
            out['x_bytes'] = e4m3fn_bytes(x0 / s.astype(np.float64))
            out['x_scale'] = s
        else:
            out[k] = v
    return out


def reference(x_bytes, x_scale, w1, b1, w2, b2, gamma, beta):
    return core(e4m3fn_values(x_bytes) * x_scale.astype(np.float64), w1, b1, w2, b2, gamma, beta)

@@ -1,0 +1,388 @@
+from contextlib import ExitStack
+
+import concourse.mybir as mybir
+from concourse.masks import make_identity
+
+F32 = mybir.dt.float32
+BF16 = mybir.dt.bfloat16
+U32 = mybir.dt.uint32
+U8 = mybir.dt.uint8
+FP8 = mybir.dt.float8_e4m3fn
+FP8X4 = mybir.dt.float8_e4m3fn_x4
+ALU = mybir.AluOpType
+ACT = mybir.ActivationFunctionType
+
+P = 128
+ROWS = 1024
+K = 512
+CH = 512
+NB = 8
+SLOPE = 0.01
+EPS = 1e-5
+BY_STATS = (3,)
+FLOPS = 2 * 2 * ROWS * K * CH
+
+
+def tile_attention_prop_pa_kernel(tc, x_bytes, x_scale, w1, b1, w2, b2, gamma, beta, out):
+    nc = tc.nc
+    with ExitStack() as ctx:
+        keep = ctx.enter_context(tc.tile_pool(name="keep", bufs=1))
+        work = ctx.enter_context(tc.tile_pool(name="work", bufs=4))
+        stage = ctx.enter_context(tc.tile_pool(name="stage", bufs=8))
+        ps_tr = ctx.enter_context(tc.psum_pool(name="ps_tr", bufs=2))
+        ps_mm = ctx.enter_context(tc.psum_pool(name="ps_mm", bufs=6))
+        ctx.enter_context(tc.manual_schedule())
+
+        sc4 = keep.tile([P, 4], F32, name="sc4")
+        xb = [keep.tile([P, 2, K], U8, name="xb%d" % c, align_bytes=64) for c in range(4)]
+        w1_raw = keep.tile([P, 4, CH], BF16, name="w1_raw", align_bytes=64)
+        w2_raw = keep.tile([P, 4, CH], BF16, name="w2_raw", align_bytes=64)
+        w1_grp = [keep.tile([P, 1024], BF16, name="w1_grp%d" % i, align_bytes=64) for i in range(2)]
+        w2_grp = [keep.tile([P, 1024], BF16, name="w2_grp%d" % i, align_bytes=64) for i in range(2)]
+        w1_q = [keep.tile([P, 256], U32, name="w1_q%d" % i, align_bytes=64) for i in range(2)]
+        w2_q = [keep.tile([P, 256], U32, name="w2_q%d" % i, align_bytes=64) for i in range(2)]
+        w1_s = [keep.tile([P, 256], U8, name="w1_s%d" % i, align_bytes=64) for i in range(2)]
+        w2_s = [keep.tile([P, 256], U8, name="w2_s%d" % i, align_bytes=64) for i in range(2)]
+        x_q = [keep.tile([P, 512], U32, name="x_q%d" % i, align_bytes=64) for i in range(2)]
+        x_s = [keep.tile([P, 512], U8, name="x_s%d" % i, align_bytes=64) for i in range(2)]
+        h_q = [keep.tile([P, 512], U32, name="h_q%d" % i, align_bytes=64) for i in range(2)]
+        h_s = [keep.tile([P, 512], U8, name="h_s%d" % i, align_bytes=64) for i in range(2)]
+        h2 = [keep.tile([P, ROWS], F32, name="h2_%d" % m, align_bytes=64) for m in range(4)]
+        y = [keep.tile([P, ROWS], F32, name="y_%d" % m, align_bytes=64) for m in range(4)]
+        stats = [keep.tile([P, 2, 6], F32, name="stats%d" % m) for m in range(4)]
+        mv = [keep.tile([P, 2], F32, name="mv%d" % m) for m in range(4)]
+        small = [keep.tile([P, 8], F32, name="small%d" % m) for m in range(4)]
+        b1_c = keep.tile([P, 4], BF16, name="b1_c")
+        rows = keep.tile([P, P], BF16, name="rows")
+        cols = keep.tile([P, 12], F32, name="cols")
+        shift = keep.tile([P, 4], F32, name="shift")
+        b_hi = keep.tile([P, 4], F32, name="b_hi")
+        b_lo = keep.tile([P, 4], F32, name="b_lo")
+        sums = [keep.tile([P, 2], F32, name="sums%d" % m) for m in range(4)]
+        squares = [keep.tile([P, 2], F32, name="squares%d" % m) for m in range(4)]
+        ident = keep.tile([P, P], F32, name="ident")
+        ident_b = keep.tile([P, P], BF16, name="ident_b")
+        half = keep.tile([P, 1], F32, name="half")
+        dummy = keep.tile([P, 1], F32, name="dummy")
+
+        x_view = x_bytes.rearrange("(p b) k -> p b k", b=NB)
+        out_view = out.rearrange("(p b) c -> p b c", b=NB)
+
+        nc.sync.dma_start(out=sc4[:], in_=x_scale.rearrange("o (p t) -> p (o t)", t=4))
+        nc.sync.dma_start(out=xb[0][:], in_=x_view[:, 0:2, :])
+        nc.sync.dma_start(out=xb[1][:], in_=x_view[:, 2:4, :])
+        nc.sync.dma_start(out=xb[2][:], in_=x_view[:, 4:6, :])
+        nc.sync.dma_start(out=xb[3][:], in_=x_view[:, 6:8, :])
+        nc.sync.dma_start(out=w1_raw[:], in_=w1.rearrange("(p j) c -> p j c", j=4))
+        nc.sync.dma_start(out=w2_raw[:], in_=w2.rearrange("(p j) c -> p j c", j=4))
+
+        nc.vector.memset(half[:], -0.5)
+        nc.vector.memset(rows[:], 0.0)
+        nc.scalar.activation(out=dummy[:], in_=half[:], func=ACT.Abs_reciprocal_sqrt)
+        make_identity(nc, ident[:])
+        nc.vector.tensor_copy(out=ident_b[:], in_=ident[:])
+        nc.scalar.dma_start(out=b1_c[:], in_=b1.rearrange("(p t) -> p t", t=4))
+        nc.scalar.dma_start(out=rows[0:4, :], in_=b2.rearrange("(m p) -> m p", p=P))
+        nc.scalar.dma_start(out=rows[4:8, :], in_=gamma.rearrange("(m p) -> m p", p=P))
+        nc.scalar.dma_start(out=rows[8:12, :], in_=beta.rearrange("(m p) -> m p", p=P))
+
+        xw = {}
+        ps = {}
+        xg = {}
+        v1 = {}
+        hg = {}
+        u2 = {}
+
+        def widen(c, eng):
+            t = work.tile([P, 2 * K], BF16, name="x_w", align_bytes=64)
+            src = xb[c][:].rearrange("p b k -> p (b k)").bitcast(FP8)
+            if eng == "act":
+                nc.scalar.copy(out=t[:], in_=src)
+            else:
+                nc.vector.tensor_copy(out=t[:], in_=src)
+            xw[c] = t
+
+        def turn_x(c):
+            pt = ps_tr.tile([P, 2, 256], F32, name="tr")
+            words = xw[c][:].bitcast(F32)
+            for b in range(2):
+                for u in range(2):
+                    nc.tensor.transpose(
+                        pt[:, u, P * b : P * b + P], words[:, 256 * b + u : 256 * b + 256 : 2], ident[:]
+                    )
+            ps["x", c] = pt
+
+        def scale_x(c):
+            g = work.tile([P, 1024], BF16, name="x_g", align_bytes=64)
+            nc.vector.tensor_tensor(
+                out=g[:].rearrange("p (r u e) -> p r u e", u=2, e=2),
+                in0=ps["x", c][:].bitcast(BF16).rearrange("p u (r e) -> p r u e", e=2),
+                in1=sc4[:].rearrange("p (o u e) -> p o u e", o=1, u=2).to_broadcast([P, 256, 2, 2]),
+                op=ALU.mult,
+            )
+            xg[c] = g
+
+        def quant_x(c):
+            cs = slice(256 * (c % 2), 256 * (c % 2) + 256)
+            nc.vector.quantize_mx(out=x_q[c // 2][:, cs].bitcast(FP8X4), scales=x_s[c // 2][:, cs], in_=xg[c][:])
+
+        def group_w1(i, eng):
+            dst = w1_grp[i][:].rearrange("p (t m j) -> p t m j", t=2, j=4)
+            src = w1_raw[:].rearrange("p j (m t) -> p t m j", t=4)[:, 2 * i : 2 * i + 2, :, :]
+            if eng == "act":
+                nc.scalar.copy(out=dst, in_=src)
+            else:
+                for t in range(2):
+                    nc.gpsimd.tensor_scalar(
+                        out=dst[:, t, :, :], in0=src[:, t, :, :], scalar1=1.0, scalar2=0.0, op0=ALU.mult, op1=ALU.add
+                    )
+
+        def quant_w1(i):
+            nc.vector.quantize_mx(out=w1_q[i][:].bitcast(FP8X4), scales=w1_s[i][:], in_=w1_grp[i][:])
+
+        def group_w2(q, eng):
+            dst = w2_grp[q // 2][:, 512 * (q % 2) : 512 * (q % 2) + 512].rearrange("p (c j) -> p c j", j=4)
+            src = w2_raw[:, :, P * q : P * q + P].rearrange("p j c -> p c j")
+            if eng == "act":
+                nc.scalar.copy(out=dst, in_=src)
+            else:
+                nc.gpsimd.tensor_scalar(out=dst, in0=src, scalar1=1.0, scalar2=0.0, op0=ALU.mult, op1=ALU.add)
+
+        def quant_w2(i):
+            nc.vector.quantize_mx(out=w2_q[i][:].bitcast(FP8X4), scales=w2_s[i][:], in_=w2_grp[i][:])
+
+        def layer1(h):
+            v = work.tile([P, 4, 512], F32, name="v1", align_bytes=64)
+            v1[h] = v
+            for t in range(4):
+                acc = ps_mm.tile([P, 512], F32, name="mm")
+                ts = slice(P * (t % 2), P * (t % 2) + P)
+                nc.tensor.matmul_mx(
+                    out=acc[:],
+                    lhsT=w1_q[t // 2][:, ts].bitcast(FP8X4),
+                    lhsT_scale=w1_s[t // 2][:, ts],
+                    rhs=x_q[h][:].bitcast(FP8X4),
+                    rhs_scale=x_s[h][:],
+                    start=True,
+                    stop=True,
+                )
+                nc.scalar.activation(out=v[:, t, :], in_=acc[:], func=ACT.Identity, bias=b1_c[:, t : t + 1])
+
+        def leaky1(c):
+            g = work.tile([P, 1024], BF16, name="h_g", align_bytes=64)
+            v = v1[c // 2][:, :, 256 * (c % 2) : 256 * (c % 2) + 256].rearrange("p t n -> p n t")
+            nc.vector.scalar_tensor_tensor(
+                out=g[:].rearrange("p (n t) -> p n t", t=4), in0=v, scalar=SLOPE, in1=v, op0=ALU.mult, op1=ALU.max
+            )
+            hg[c] = g
+
+        def quant_h(c):
+            cs = slice(256 * (c % 2), 256 * (c % 2) + 256)
+            nc.vector.quantize_mx(out=h_q[c // 2][:, cs].bitcast(FP8X4), scales=h_s[c // 2][:, cs], in_=hg[c][:])
+
+        def layer2(m, h):
+            acc = ps_mm.tile([P, 512], F32, name="mm")
+            ms = slice(P * (m % 2), P * (m % 2) + P)
+            nc.tensor.matmul_mx(
+                out=acc[:],
+                lhsT=w2_q[m // 2][:, ms].bitcast(FP8X4),
+                lhsT_scale=w2_s[m // 2][:, ms],
+                rhs=h_q[h][:].bitcast(FP8X4),
+                rhs_scale=h_s[h][:],
+                start=True,
+                stop=True,
+            )
+            ps[m, h] = acc
+            u = work.tile([P, 512], F32, name="u2", align_bytes=64)
+            nc.scalar.activation(out=u[:], in_=acc[:], func=ACT.Identity, bias=b_lo[:, m : m + 1], scale=SLOPE)
+            u2[m, h] = u
+
+        def leaky2(m, h):
+            nc.vector.scalar_tensor_tensor(
+                out=h2[m][:, 512 * h : 512 * h + 512],
+                in0=ps[m, h][:],
+                scalar=b_hi[:, m : m + 1],
+                in1=u2[m, h][:],
+                op0=ALU.add,
+                op1=ALU.max,
+                accum_out=None if m in BY_STATS else sums[m][:, h : h + 1],
+            )
+
+        def square(m, h):
+            junk = work.tile([P, 512], F32, name="junk", align_bytes=64)
+            nc.scalar.activation(
+                out=junk[:],
+                in_=h2[m][:, 512 * h : 512 * h + 512],
+                func=ACT.Square,
+                scale=1.0 / 32.0,
+                accum_out=squares[m][:, h : h + 1],
+            )
+
+        def mean_part(m):
+            s = small[m]
+            nc.gpsimd.tensor_scalar(out=s[:, 3:4], in0=squares[m][:, 0:1], scalar1=EPS, scalar2=None, op0=ALU.add)
+            nc.gpsimd.tensor_scalar(
+                out=mv[m][:, 0:1], in0=sums[m][:, 0:1], scalar1=sums[m][:, 1:2], scalar2=1.0 / ROWS, op0=ALU.add, op1=ALU.mult
+            )
+            nc.gpsimd.tensor_tensor(out=s[:, 5:6], in0=mv[m][:, 0:1], in1=mv[m][:, 0:1], op=ALU.mult)
+            nc.gpsimd.tensor_tensor(out=s[:, 4:5], in0=s[:, 3:4], in1=s[:, 5:6], op=ALU.subtract)
+
+        def deviation(m):
+            nc.scalar.activation(
+                out=small[m][:, 0:1], in_=squares[m][:, 1:2], func=ACT.Abs_reciprocal_sqrt, bias=small[m][:, 4:5]
+            )
+
+        def stat(m, h):
+            nc.vector.bn_stats(out=stats[m][:, h, :], in_=h2[m][:, 512 * h : 512 * h + 512])
+
+        def aggregate(m):
+            nc.vector.bn_aggr(out=mv[m][:], in_=stats[m][:].rearrange("p a b -> p (a b)"))
+            nc.scalar.activation(
+                out=small[m][:, 0:1], in_=mv[m][:, 1:2], func=ACT.Abs_reciprocal_sqrt, bias=EPS
+            )
+
+        def coeff_a(m):
+            s = small[m]
+            nc.vector.tensor_tensor(out=s[:, 1:2], in0=s[:, 0:1], in1=cols[:, 4 + m : 5 + m], op=ALU.mult)
+
+        def coeff_b(m):
+            s = small[m]
+            nc.vector.scalar_tensor_tensor(
+                out=s[:, 2:3], in0=mv[m][:, 0:1], scalar=s[:, 1:2], in1=cols[:, 8 + m : 9 + m], op0=ALU.mult, op1=ALU.subtract
+            )
+
+        def norm(m, h, eng):
+            hs = slice(512 * h, 512 * h + 512)
+            e = nc.gpsimd if eng == "pool" else nc.vector
+            e.tensor_scalar(
+                out=y[m][:, hs],
+                in0=h2[m][:, hs],
+                scalar1=small[m][:, 1:2],
+                scalar2=small[m][:, 2:3],
+                op0=ALU.mult,
+                op1=ALU.subtract,
+            )
+
+        def turn_y(m, h):
+            if m == 0:
+                pt = ps_tr.tile([P, 4, P], F32, name="tr")
+            else:
+                pt = ps_mm.tile([P, 4, P], F32, name="mm")
+            for b in range(4):
+                col = 512 * h + P * b
+                nc.tensor.transpose(pt[:, b, :], y[m][:, col : col + P], ident[:])
+            ps["y", m, h] = pt
+
+        def copy_y(m, h, eng):
+            o = stage.tile([P, 4, P], F32, name="o_sb", align_bytes=64)
+            if eng == "act":
+                nc.scalar.copy(out=o[:], in_=ps["y", m, h][:])
+            else:
+                nc.vector.tensor_copy(out=o[:], in_=ps["y", m, h][:])
+            nc.sync.dma_start(out=out_view[:, 4 * h : 4 * h + 4, P * m : P * m + P], in_=o[:])
+
+        widen(0, "dve")
+        widen(1, "act")
+        widen(2, "dve")
+        widen(3, "act")
+        turn_x(0)
+        turn_x(1)
+        scale_x(0)
+        turn_x(2)
+        scale_x(1)
+        turn_x(3)
+        group_w1(1, "pool")
+        group_w1(0, "act")
+        quant_x(0)
+        quant_x(1)
+        ps_c = ps_mm.tile([P, P], BF16, name="mm")
+        nc.tensor.transpose(ps_c[:], rows[:], ident_b[:])
+        quant_w1(1)
+        quant_w1(0)
+        for q in range(4):
+            group_w2(q, "pool")
+        layer1(0)
+        scale_x(2)
+        nc.vector.tensor_copy(out=cols[:], in_=ps_c[:, 0:12])
+        scale_x(3)
+        quant_x(2)
+        quant_x(3)
+        layer1(1)
+        nc.vector.scalar_tensor_tensor(
+            out=shift[:], in0=cols[:, 0:4], scalar=SLOPE, in1=cols[:, 0:4], op0=ALU.mult, op1=ALU.max
+        )
+        leaky1(0)
+        nc.vector.tensor_tensor(out=b_hi[:], in0=cols[:, 0:4], in1=shift[:], op=ALU.subtract)
+        leaky1(1)
+        nc.vector.scalar_tensor_tensor(
+            out=b_lo[:], in0=cols[:, 0:4], scalar=SLOPE, in1=shift[:], op0=ALU.mult, op1=ALU.subtract
+        )
+        quant_h(0)
+        quant_w2(0)
+        quant_h(1)
+        quant_w2(1)
+        for m in range(4):
+            layer2(m, 0)
+        leaky1(2)
+        leaky1(3)
+        quant_h(2)
+        leaky2(0, 0)
+        quant_h(3)
+        leaky2(1, 0)
+        square(0, 0)
+        layer2(0, 1)
+        leaky2(2, 0)
+        layer2(1, 1)
+        square(1, 0)
+        leaky2(0, 1)
+        square(0, 1)
+        mean_part(0)
+        layer2(2, 1)
+        leaky2(1, 1)
+        deviation(0)
+        square(1, 1)
+        leaky2(3, 0)
+        coeff_a(0)
+        mean_part(1)
+        layer2(3, 1)
+        stat(3, 0)
+        coeff_b(0)
+        deviation(1)
+        leaky2(2, 1)
+        norm(0, 0, "dve")
+        norm(0, 1, "pool")
+        coeff_a(1)
+        turn_y(0, 0)
+        square(2, 0)
+        leaky2(3, 1)
+        coeff_b(1)
+        turn_y(0, 1)
+        copy_y(0, 0, "act")
+        square(2, 1)
+        mean_part(2)
+        norm(1, 0, "dve")
+        norm(1, 1, "pool")
+        stat(3, 1)
+        copy_y(0, 1, "act")
+        turn_y(1, 0)
+        deviation(2)
+        turn_y(1, 1)
+        copy_y(1, 0, "act")
+        aggregate(3)
+        coeff_a(2)
+        copy_y(1, 1, "dve")
+        coeff_b(2)
+        coeff_a(3)
+        norm(2, 0, "dve")
+        coeff_b(3)
+        norm(2, 1, "dve")
+        norm(3, 0, "dve")
+        norm(3, 1, "pool")
+        turn_y(2, 0)
+        turn_y(2, 1)
+        copy_y(2, 0, "act")
+        copy_y(2, 1, "dve")
+        turn_y(3, 0)
+        turn_y(3, 1)
+        copy_y(3, 0, "act")
+        copy_y(3, 1, "dve")

@@ -34,7 +34,8 @@ def tile_attention_prop_pa_kernel(tc, x_bytes, x_scale, w1, b1, w2, b2, gamma, b
         ctx.enter_context(tc.manual_schedule())
 
         sc4 = keep.tile([P, 4], F32, name="sc4")
-        xb = [keep.tile([P, 2, K], U8, name="xb%d" % c, align_bytes=64) for c in range(4)]
+        x_first = [keep.tile([P, 2, K], U8, name="x_first%d" % c, align_bytes=64) for c in range(2)]
+        x_rest = keep.tile([P, 4, K], U8, name="x_rest", align_bytes=64)
         w1_raw = keep.tile([P, 4, CH], BF16, name="w1_raw", align_bytes=64)
         w2_raw = keep.tile([P, 4, CH], BF16, name="w2_raw", align_bytes=64)
         w1_grp = [keep.tile([P, 1024], BF16, name="w1_grp%d" % i, align_bytes=64) for i in range(2)]
@@ -55,7 +56,6 @@ def tile_attention_prop_pa_kernel(tc, x_bytes, x_scale, w1, b1, w2, b2, gamma, b
         b1_c = keep.tile([P, 4], BF16, name="b1_c")
         rows = keep.tile([P, P], BF16, name="rows")
         cols = keep.tile([P, 12], F32, name="cols")
-        shift = keep.tile([P, 4], F32, name="shift")
         b_hi = keep.tile([P, 4], F32, name="b_hi")
         b_lo = keep.tile([P, 4], F32, name="b_lo")
         sums = [keep.tile([P, 2], F32, name="sums%d" % m) for m in range(4)]
@@ -69,33 +69,33 @@ def tile_attention_prop_pa_kernel(tc, x_bytes, x_scale, w1, b1, w2, b2, gamma, b
         out_view = out.rearrange("(p b) c -> p b c", b=NB)
 
         nc.sync.dma_start(out=sc4[:], in_=x_scale.rearrange("o (p t) -> p (o t)", t=4))
-        nc.sync.dma_start(out=xb[0][:], in_=x_view[:, 0:2, :])
-        nc.sync.dma_start(out=xb[1][:], in_=x_view[:, 2:4, :])
-        nc.sync.dma_start(out=xb[2][:], in_=x_view[:, 4:6, :])
-        nc.sync.dma_start(out=xb[3][:], in_=x_view[:, 6:8, :])
-        nc.sync.dma_start(out=w1_raw[:], in_=w1.rearrange("(p j) c -> p j c", j=4))
-        nc.sync.dma_start(out=w2_raw[:], in_=w2.rearrange("(p j) c -> p j c", j=4))
-
-        nc.vector.memset(half[:], -0.5)
+        nc.sync.dma_start(out=x_first[0][:], in_=x_view[:, 0:2, :])
+        nc.sync.dma_start(out=x_first[1][:], in_=x_view[:, 2:4, :])
+        nc.sync.dma_start(out=x_rest[:], in_=x_view[:, 4:8, :])
         nc.vector.memset(rows[:], 0.0)
-        nc.scalar.activation(out=dummy[:], in_=half[:], func=ACT.Abs_reciprocal_sqrt)
-        make_identity(nc, ident[:])
-        nc.vector.tensor_copy(out=ident_b[:], in_=ident[:])
+        nc.vector.memset(half[:], 1.0)
         nc.scalar.dma_start(out=b1_c[:], in_=b1.rearrange("(p t) -> p t", t=4))
+        nc.scalar.activation(out=dummy[:], in_=half[:], func=ACT.Abs_reciprocal_sqrt)
+        nc.sync.dma_start(out=w1_raw[:], in_=w1.rearrange("(p j) c -> p j c", j=4))
         nc.scalar.dma_start(out=rows[0:4, :], in_=b2.rearrange("(m p) -> m p", p=P))
         nc.scalar.dma_start(out=rows[4:8, :], in_=gamma.rearrange("(m p) -> m p", p=P))
         nc.scalar.dma_start(out=rows[8:12, :], in_=beta.rearrange("(m p) -> m p", p=P))
+        nc.sync.dma_start(out=w2_raw[:], in_=w2.rearrange("(p j) c -> p j c", j=4))
+        make_identity(nc, ident[:])
+        nc.vector.tensor_copy(out=ident_b[:], in_=ident[:])
 
         xw = {}
         ps = {}
         xg = {}
-        v1 = {}
+        v1 = [keep.tile([P, 4, 512], F32, name="v1_%d" % h, align_bytes=64) for h in range(2)]
         hg = {}
         u2 = {}
 
         def widen(c, eng):
             t = work.tile([P, 2 * K], BF16, name="x_w", align_bytes=64)
-            src = xb[c][:].rearrange("p b k -> p (b k)").bitcast(FP8)
+            src = x_first[c] if c < 2 else x_rest
+            b0 = 0 if c < 2 else 2 * c - 4
+            src = src[:, b0 : b0 + 2, :].rearrange("p b k -> p (b k)").bitcast(FP8)
             if eng == "act":
                 nc.scalar.copy(out=t[:], in_=src)
             else:
@@ -131,6 +131,8 @@ def tile_attention_prop_pa_kernel(tc, x_bytes, x_scale, w1, b1, w2, b2, gamma, b
             src = w1_raw[:].rearrange("p j (m t) -> p t m j", t=4)[:, 2 * i : 2 * i + 2, :, :]
             if eng == "act":
                 nc.scalar.copy(out=dst, in_=src)
+            elif eng == "dve":
+                nc.vector.tensor_copy(out=dst, in_=src)
             else:
                 for t in range(2):
                     nc.gpsimd.tensor_scalar(
@@ -145,28 +147,47 @@ def tile_attention_prop_pa_kernel(tc, x_bytes, x_scale, w1, b1, w2, b2, gamma, b
             src = w2_raw[:, :, P * q : P * q + P].rearrange("p j c -> p c j")
             if eng == "act":
                 nc.scalar.copy(out=dst, in_=src)
+            elif eng == "dve":
+                nc.vector.tensor_copy(out=dst, in_=src)
             else:
                 nc.gpsimd.tensor_scalar(out=dst, in0=src, scalar1=1.0, scalar2=0.0, op0=ALU.mult, op1=ALU.add)
 
         def quant_w2(i):
             nc.vector.quantize_mx(out=w2_q[i][:].bitcast(FP8X4), scales=w2_s[i][:], in_=w2_grp[i][:])
 
-        def layer1(h):
-            v = work.tile([P, 4, 512], F32, name="v1", align_bytes=64)
-            v1[h] = v
-            for t in range(4):
-                acc = ps_mm.tile([P, 512], F32, name="mm")
-                ts = slice(P * (t % 2), P * (t % 2) + P)
-                nc.tensor.matmul_mx(
-                    out=acc[:],
-                    lhsT=w1_q[t // 2][:, ts].bitcast(FP8X4),
-                    lhsT_scale=w1_s[t // 2][:, ts],
-                    rhs=x_q[h][:].bitcast(FP8X4),
-                    rhs_scale=x_s[h][:],
-                    start=True,
-                    stop=True,
-                )
-                nc.scalar.activation(out=v[:, t, :], in_=acc[:], func=ACT.Identity, bias=b1_c[:, t : t + 1])
+        def turn_rows():
+            ps["rows"] = ps_mm.tile([P, P], BF16, name="mm")
+            nc.tensor.transpose(ps["rows"][:], rows[:], ident_b[:])
+
+        def columns():
+            nc.vector.tensor_copy(out=cols[:], in_=ps["rows"][:, 0:12])
+
+        def bounds():
+            nc.vector.tensor_scalar(
+                out=b_hi[:], in0=cols[:, 0:4], scalar1=1.0 - SLOPE, scalar2=0.0, op0=ALU.mult, op1=ALU.min
+            )
+            nc.vector.tensor_scalar(
+                out=b_lo[:], in0=cols[:, 0:4], scalar1=SLOPE - 1.0, scalar2=0.0, op0=ALU.mult, op1=ALU.min
+            )
+
+        def mm1(h, t):
+            acc = ps_mm.tile([P, 512], F32, name="mm")
+            ts = slice(P * (t % 2), P * (t % 2) + P)
+            nc.tensor.matmul_mx(
+                out=acc[:],
+                lhsT=w1_q[t // 2][:, ts].bitcast(FP8X4),
+                lhsT_scale=w1_s[t // 2][:, ts],
+                rhs=x_q[h][:].bitcast(FP8X4),
+                rhs_scale=x_s[h][:],
+                start=True,
+                stop=True,
+            )
+            ps["h", h, t] = acc
+
+        def bias1(h, t):
+            nc.scalar.activation(
+                out=v1[h][:, t, :], in_=ps["h", h, t][:], func=ACT.Identity, bias=b1_c[:, t : t + 1]
+            )
 
         def leaky1(c):
             g = work.tile([P, 1024], BF16, name="h_g", align_bytes=64)
@@ -180,7 +201,7 @@ def tile_attention_prop_pa_kernel(tc, x_bytes, x_scale, w1, b1, w2, b2, gamma, b
             cs = slice(256 * (c % 2), 256 * (c % 2) + 256)
             nc.vector.quantize_mx(out=h_q[c // 2][:, cs].bitcast(FP8X4), scales=h_s[c // 2][:, cs], in_=hg[c][:])
 
-        def layer2(m, h):
+        def mm2(m, h):
             acc = ps_mm.tile([P, 512], F32, name="mm")
             ms = slice(P * (m % 2), P * (m % 2) + P)
             nc.tensor.matmul_mx(
@@ -193,8 +214,10 @@ def tile_attention_prop_pa_kernel(tc, x_bytes, x_scale, w1, b1, w2, b2, gamma, b
                 stop=True,
             )
             ps[m, h] = acc
-            u = work.tile([P, 512], F32, name="u2", align_bytes=64)
-            nc.scalar.activation(out=u[:], in_=acc[:], func=ACT.Identity, bias=b_lo[:, m : m + 1], scale=SLOPE)
+
+        def low2(m, h):
+            u = stage.tile([P, 512], F32, name="u2", align_bytes=64)
+            nc.scalar.activation(out=u[:], in_=ps[m, h][:], func=ACT.Identity, bias=b_lo[:, m : m + 1], scale=SLOPE)
             u2[m, h] = u
 
         def leaky2(m, h):
@@ -208,38 +231,42 @@ def tile_attention_prop_pa_kernel(tc, x_bytes, x_scale, w1, b1, w2, b2, gamma, b
                 accum_out=None if m in BY_STATS else sums[m][:, h : h + 1],
             )
 
-        def square(m, h):
-            junk = work.tile([P, 512], F32, name="junk", align_bytes=64)
-            nc.scalar.activation(
-                out=junk[:],
-                in_=h2[m][:, 512 * h : 512 * h + 512],
-                func=ACT.Square,
-                scale=1.0 / 32.0,
-                accum_out=squares[m][:, h : h + 1],
-            )
-
-        def mean_part(m):
-            s = small[m]
-            nc.gpsimd.tensor_scalar(out=s[:, 3:4], in0=squares[m][:, 0:1], scalar1=EPS, scalar2=None, op0=ALU.add)
-            nc.gpsimd.tensor_scalar(
-                out=mv[m][:, 0:1], in0=sums[m][:, 0:1], scalar1=sums[m][:, 1:2], scalar2=1.0 / ROWS, op0=ALU.add, op1=ALU.mult
-            )
-            nc.gpsimd.tensor_tensor(out=s[:, 5:6], in0=mv[m][:, 0:1], in1=mv[m][:, 0:1], op=ALU.mult)
-            nc.gpsimd.tensor_tensor(out=s[:, 4:5], in0=s[:, 3:4], in1=s[:, 5:6], op=ALU.subtract)
-
-        def deviation(m):
-            nc.scalar.activation(
-                out=small[m][:, 0:1], in_=squares[m][:, 1:2], func=ACT.Abs_reciprocal_sqrt, bias=small[m][:, 4:5]
-            )
-
         def stat(m, h):
-            nc.vector.bn_stats(out=stats[m][:, h, :], in_=h2[m][:, 512 * h : 512 * h + 512])
+            src = h2[m][:, 512 * h : 512 * h + 512]
+            if m in BY_STATS:
+                nc.vector.bn_stats(out=stats[m][:, h, :], in_=src)
+            else:
+                junk = work.tile([P, 512], F32, name="junk", align_bytes=64)
+                nc.scalar.activation(
+                    out=junk[:], in_=src, func=ACT.Square, scale=1.0 / 32.0, accum_out=squares[m][:, h : h + 1]
+                )
 
         def aggregate(m):
-            nc.vector.bn_aggr(out=mv[m][:], in_=stats[m][:].rearrange("p a b -> p (a b)"))
-            nc.scalar.activation(
-                out=small[m][:, 0:1], in_=mv[m][:, 1:2], func=ACT.Abs_reciprocal_sqrt, bias=EPS
-            )
+            s = small[m]
+            if m in BY_STATS:
+                nc.vector.bn_aggr(out=mv[m][:], in_=stats[m][:].rearrange("p a b -> p (a b)"))
+            else:
+                nc.gpsimd.tensor_scalar(out=s[:, 3:4], in0=squares[m][:, 0:1], scalar1=EPS, scalar2=None, op0=ALU.add)
+                nc.gpsimd.tensor_scalar(
+                    out=s[:, 6:7],
+                    in0=sums[m][:, 0:1],
+                    scalar1=sums[m][:, 1:2],
+                    scalar2=-1.0 / ROWS,
+                    op0=ALU.add,
+                    op1=ALU.mult,
+                )
+                nc.gpsimd.tensor_tensor(out=s[:, 5:6], in0=s[:, 6:7], in1=s[:, 6:7], op=ALU.mult)
+                nc.gpsimd.tensor_tensor(out=s[:, 4:5], in0=s[:, 3:4], in1=s[:, 5:6], op=ALU.subtract)
+
+        def deviation(m):
+            s = small[m]
+            if m in BY_STATS:
+                nc.scalar.activation(out=s[:, 0:1], in_=mv[m][:, 1:2], func=ACT.Abs_reciprocal_sqrt, bias=EPS)
+                nc.scalar.activation(out=s[:, 6:7], in_=mv[m][:, 0:1], func=ACT.Identity, scale=-1.0)
+            else:
+                nc.scalar.activation(
+                    out=s[:, 0:1], in_=squares[m][:, 1:2], func=ACT.Abs_reciprocal_sqrt, bias=s[:, 4:5]
+                )
 
         def coeff_a(m):
             s = small[m]
@@ -248,26 +275,24 @@ def tile_attention_prop_pa_kernel(tc, x_bytes, x_scale, w1, b1, w2, b2, gamma, b
         def coeff_b(m):
             s = small[m]
             nc.vector.scalar_tensor_tensor(
-                out=s[:, 2:3], in0=mv[m][:, 0:1], scalar=s[:, 1:2], in1=cols[:, 8 + m : 9 + m], op0=ALU.mult, op1=ALU.subtract
+                out=s[:, 2:3], in0=s[:, 6:7], scalar=s[:, 1:2], in1=cols[:, 8 + m : 9 + m], op0=ALU.mult, op1=ALU.add
             )
 
         def norm(m, h, eng):
             hs = slice(512 * h, 512 * h + 512)
-            e = nc.gpsimd if eng == "pool" else nc.vector
-            e.tensor_scalar(
-                out=y[m][:, hs],
-                in0=h2[m][:, hs],
-                scalar1=small[m][:, 1:2],
-                scalar2=small[m][:, 2:3],
-                op0=ALU.mult,
-                op1=ALU.subtract,
-            )
+            s = small[m]
+            if eng == "act":
+                nc.scalar.activation(
+                    out=y[m][:, hs], in_=h2[m][:, hs], func=ACT.Identity, bias=s[:, 2:3], scale=s[:, 1:2]
+                )
+            else:
+                e = nc.gpsimd if eng == "pool" else nc.vector
+                e.tensor_scalar(
+                    out=y[m][:, hs], in0=h2[m][:, hs], scalar1=s[:, 1:2], scalar2=s[:, 2:3], op0=ALU.mult, op1=ALU.add
+                )
 
         def turn_y(m, h):
-            if m == 0:
-                pt = ps_tr.tile([P, 4, P], F32, name="tr")
-            else:
-                pt = ps_mm.tile([P, 4, P], F32, name="mm")
+            pt = ps_mm.tile([P, 4, P], F32, name="mm")
             for b in range(4):
                 col = 512 * h + P * b
                 nc.tensor.transpose(pt[:, b, :], y[m][:, col : col + P], ident[:])
@@ -281,108 +306,128 @@ def tile_attention_prop_pa_kernel(tc, x_bytes, x_scale, w1, b1, w2, b2, gamma, b
                 nc.vector.tensor_copy(out=o[:], in_=ps["y", m, h][:])
             nc.sync.dma_start(out=out_view[:, 4 * h : 4 * h + 4, P * m : P * m + P], in_=o[:])
 
+        widen(2, "act")
         widen(0, "dve")
-        widen(1, "act")
-        widen(2, "dve")
-        widen(3, "act")
+        widen(1, "dve")
+        group_w1(0, "pool")
         turn_x(0)
         turn_x(1)
         scale_x(0)
-        turn_x(2)
         scale_x(1)
-        turn_x(3)
-        group_w1(1, "pool")
-        group_w1(0, "act")
-        quant_x(0)
-        quant_x(1)
-        ps_c = ps_mm.tile([P, P], BF16, name="mm")
-        nc.tensor.transpose(ps_c[:], rows[:], ident_b[:])
+        group_w1(1, "act")
         quant_w1(1)
+        turn_x(2)
+        widen(3, "act")
+        turn_rows()
+        quant_x(1)
+        columns()
+        group_w2(0, "act")
+        group_w2(3, "act")
+        turn_x(3)
+        quant_x(0)
         quant_w1(0)
-        for q in range(4):
-            group_w2(q, "pool")
-        layer1(0)
         scale_x(2)
-        nc.vector.tensor_copy(out=cols[:], in_=ps_c[:, 0:12])
+        group_w2(2, "act")
+        group_w2(1, "act")
         scale_x(3)
+        mm1(0, 2)
+        mm1(0, 0)
+        bias1(0, 2)
+        mm1(0, 1)
         quant_x(2)
         quant_x(3)
-        layer1(1)
-        nc.vector.scalar_tensor_tensor(
-            out=shift[:], in0=cols[:, 0:4], scalar=SLOPE, in1=cols[:, 0:4], op0=ALU.mult, op1=ALU.max
-        )
-        leaky1(0)
-        nc.vector.tensor_tensor(out=b_hi[:], in0=cols[:, 0:4], in1=shift[:], op=ALU.subtract)
-        leaky1(1)
-        nc.vector.scalar_tensor_tensor(
-            out=b_lo[:], in0=cols[:, 0:4], scalar=SLOPE, in1=shift[:], op0=ALU.mult, op1=ALU.subtract
-        )
-        quant_h(0)
-        quant_w2(0)
-        quant_h(1)
+        mm1(0, 3)
+        mm1(1, 0)
+        bias1(0, 0)
         quant_w2(1)
-        for m in range(4):
-            layer2(m, 0)
+        bias1(0, 1)
+        bounds()
+        bias1(0, 3)
+        quant_w2(0)
+        leaky1(0)
+        mm1(1, 3)
+        leaky1(1)
+        bias1(1, 0)
+        quant_h(0)
+        mm1(1, 2)
+        bias1(1, 3)
+        bias1(1, 2)
+        mm1(1, 1)
+        quant_h(1)
+        mm2(0, 0)
+        mm2(1, 0)
+        mm2(3, 0)
+        bias1(1, 1)
         leaky1(2)
         leaky1(3)
         quant_h(2)
-        leaky2(0, 0)
         quant_h(3)
-        leaky2(1, 0)
-        square(0, 0)
-        layer2(0, 1)
-        leaky2(2, 0)
-        layer2(1, 1)
-        square(1, 0)
-        leaky2(0, 1)
-        square(0, 1)
-        mean_part(0)
-        layer2(2, 1)
-        leaky2(1, 1)
-        deviation(0)
-        square(1, 1)
+        low2(1, 0)
+        mm2(2, 0)
+        low2(0, 0)
+        low2(3, 0)
+        low2(2, 0)
+        leaky2(0, 0)
         leaky2(3, 0)
-        coeff_a(0)
-        mean_part(1)
-        layer2(3, 1)
+        leaky2(1, 0)
+        mm2(0, 1)
+        low2(0, 1)
+        mm2(1, 1)
+        leaky2(0, 1)
+        mm2(3, 1)
+        low2(1, 1)
+        mm2(2, 1)
+        stat(0, 0)
+        low2(3, 1)
+        stat(0, 1)
+        stat(1, 0)
+        aggregate(0)
+        leaky2(2, 0)
+        deviation(0)
+        leaky2(1, 1)
+        leaky2(3, 1)
+        low2(2, 1)
         stat(3, 0)
-        coeff_b(0)
+        coeff_a(0)
+        stat(1, 1)
+        stat(2, 0)
+        aggregate(1)
         deviation(1)
+        coeff_b(0)
         leaky2(2, 1)
         norm(0, 0, "dve")
-        norm(0, 1, "pool")
-        coeff_a(1)
-        turn_y(0, 0)
-        square(2, 0)
-        leaky2(3, 1)
-        coeff_b(1)
-        turn_y(0, 1)
-        copy_y(0, 0, "act")
-        square(2, 1)
-        mean_part(2)
-        norm(1, 0, "dve")
-        norm(1, 1, "pool")
         stat(3, 1)
-        copy_y(0, 1, "act")
-        turn_y(1, 0)
-        deviation(2)
-        turn_y(1, 1)
-        copy_y(1, 0, "act")
+        norm(0, 1, "act")
+        coeff_a(1)
+        aggregate(2)
+        turn_y(0, 0)
+        coeff_b(1)
+        stat(2, 1)
         aggregate(3)
+        norm(1, 1, "dve")
+        deviation(3)
+        norm(1, 0, "dve")
+        turn_y(0, 1)
+        deviation(2)
+        copy_y(0, 0, "act")
+        turn_y(1, 1)
         coeff_a(2)
-        copy_y(1, 1, "dve")
-        coeff_b(2)
         coeff_a(3)
-        norm(2, 0, "dve")
+        turn_y(1, 0)
+        copy_y(0, 1, "act")
+        copy_y(1, 1, "act")
+        copy_y(1, 0, "act")
+        coeff_b(2)
         coeff_b(3)
+        norm(2, 0, "dve")
         norm(2, 1, "dve")
-        norm(3, 0, "dve")
-        norm(3, 1, "pool")
         turn_y(2, 0)
+        norm(3, 0, "dve")
         turn_y(2, 1)
-        copy_y(2, 0, "act")
-        copy_y(2, 1, "dve")
+        norm(3, 1, "act")
         turn_y(3, 0)
-        turn_y(3, 1)
+        copy_y(2, 0, "dve")
+        copy_y(2, 1, "act")
         copy_y(3, 0, "act")
-        copy_y(3, 1, "dve")
+        turn_y(3, 1)
+        copy_y(3, 1, "act")

@@ -62,16 +62,18 @@ def tile_attention_prop_pa_kernel(tc, x_bytes, x_scale, w1, b1, w2, b2, gamma, b
         squares = [keep.tile([P, 2], F32, name="squares%d" % m) for m in range(4)]
         ident = keep.tile([P, P], F32, name="ident")
         ident_b = keep.tile([P, P], BF16, name="ident_b")
+        zeros = keep.tile([P, 512], BF16, name="zeros", align_bytes=64)
         half = keep.tile([P, 1], F32, name="half")
         dummy = keep.tile([P, 1], F32, name="dummy")
 
         x_view = x_bytes.rearrange("(p b) k -> p b k", b=NB)
         out_view = out.rearrange("(p b) c -> p b c", b=NB)
 
-        nc.sync.dma_start(out=sc4[:], in_=x_scale.rearrange("o (p t) -> p (o t)", t=4))
         nc.sync.dma_start(out=x_first[0][:], in_=x_view[:, 0:2, :])
+        nc.sync.dma_start(out=sc4[:], in_=x_scale.rearrange("o (p t) -> p (o t)", t=4))
         nc.sync.dma_start(out=x_first[1][:], in_=x_view[:, 2:4, :])
         nc.sync.dma_start(out=x_rest[:], in_=x_view[:, 4:8, :])
+        nc.vector.memset(zeros[:], 0.0)
         nc.vector.memset(rows[:], 0.0)
         nc.vector.memset(half[:], 1.0)
         nc.scalar.dma_start(out=b1_c[:], in_=b1.rearrange("(p t) -> p t", t=4))
@@ -91,36 +93,45 @@ def tile_attention_prop_pa_kernel(tc, x_bytes, x_scale, w1, b1, w2, b2, gamma, b
         hg = {}
         u2 = {}
 
-        def widen(c, eng):
-            t = work.tile([P, 2 * K], BF16, name="x_w", align_bytes=64)
-            src = x_first[c] if c < 2 else x_rest
-            b0 = 0 if c < 2 else 2 * c - 4
-            src = src[:, b0 : b0 + 2, :].rearrange("p b k -> p (b k)").bitcast(FP8)
+        def warm():
+            acc = ps_mm.tile([P, 512], F32, name="mm")
+            nc.tensor.matmul(acc[:], lhsT=zeros[:, 0:P], rhs=zeros[:], start=True, stop=True)
+
+        def widen(b, n, eng):
+            t = work.tile([P, n * K], BF16, name="x_w%d" % n, align_bytes=64)
+            src, b0 = (x_first[b // 2], b % 2) if b < 4 else (x_rest, b - 4)
+            src = src[:, b0 : b0 + n, :].rearrange("p b k -> p (b k)").bitcast(FP8)
             if eng == "act":
                 nc.scalar.copy(out=t[:], in_=src)
-            else:
+            elif eng == "dve":
                 nc.vector.tensor_copy(out=t[:], in_=src)
-            xw[c] = t
+            else:
+                for i in range(n):
+                    cs = slice(K * i, K * i + K)
+                    nc.gpsimd.tensor_copy(out=t[:, cs], in_=src[:, cs])
+            xw[b] = t
 
-        def turn_x(c):
-            pt = ps_tr.tile([P, 2, 256], F32, name="tr")
-            words = xw[c][:].bitcast(F32)
-            for b in range(2):
+        def turn_x(b, n):
+            pt = ps_tr.tile([P, 2, P * n], F32, name="tr")
+            words = xw[b][:].bitcast(F32)
+            for i in range(n):
                 for u in range(2):
                     nc.tensor.transpose(
-                        pt[:, u, P * b : P * b + P], words[:, 256 * b + u : 256 * b + 256 : 2], ident[:]
+                        pt[:, u, P * i : P * i + P], words[:, 256 * i + u : 256 * i + 256 : 2], ident[:]
                     )
-            ps["x", c] = pt
+            ps["x", b] = pt
 
-        def scale_x(c):
-            g = work.tile([P, 1024], BF16, name="x_g", align_bytes=64)
+        def scale_x(b, n):
+            c = b // 2
+            if c not in xg:
+                xg[c] = work.tile([P, 1024], BF16, name="x_g", align_bytes=64)
+            r0 = 512 * (b % 2)
             nc.vector.tensor_tensor(
-                out=g[:].rearrange("p (r u e) -> p r u e", u=2, e=2),
-                in0=ps["x", c][:].bitcast(BF16).rearrange("p u (r e) -> p r u e", e=2),
-                in1=sc4[:].rearrange("p (o u e) -> p o u e", o=1, u=2).to_broadcast([P, 256, 2, 2]),
+                out=xg[c][:, r0 : r0 + 512 * n].rearrange("p (r u e) -> p r u e", u=2, e=2),
+                in0=ps["x", b][:].bitcast(BF16).rearrange("p u (r e) -> p r u e", e=2),
+                in1=sc4[:].rearrange("p (o u e) -> p o u e", o=1, u=2).to_broadcast([P, P * n, 2, 2]),
                 op=ALU.mult,
             )
-            xg[c] = g
 
         def quant_x(c):
             cs = slice(256 * (c % 2), 256 * (c % 2) + 256)
@@ -143,8 +154,8 @@ def tile_attention_prop_pa_kernel(tc, x_bytes, x_scale, w1, b1, w2, b2, gamma, b
             nc.vector.quantize_mx(out=w1_q[i][:].bitcast(FP8X4), scales=w1_s[i][:], in_=w1_grp[i][:])
 
         def group_w2(q, eng):
-            dst = w2_grp[q // 2][:, 512 * (q % 2) : 512 * (q % 2) + 512].rearrange("p (c j) -> p c j", j=4)
-            src = w2_raw[:, :, P * q : P * q + P].rearrange("p j c -> p c j")
+            dst = w2_grp[q // 2][:, 512 * (q % 2) : 512 * (q % 2) + 512].rearrange("p (c i j) -> p c j i", i=4, j=4)
+            src = w2_raw[:, :, P * q : P * q + P].rearrange("p j (c i) -> p c j i", i=4)
             if eng == "act":
                 nc.scalar.copy(out=dst, in_=src)
             elif eng == "dve":
@@ -202,7 +213,10 @@ def tile_attention_prop_pa_kernel(tc, x_bytes, x_scale, w1, b1, w2, b2, gamma, b
             nc.vector.quantize_mx(out=h_q[c // 2][:, cs].bitcast(FP8X4), scales=h_s[c // 2][:, cs], in_=hg[c][:])
 
         def mm2(m, h):
-            acc = ps_mm.tile([P, 512], F32, name="mm")
+            if h == 1 and m >= 2:
+                acc = ps_tr.tile([P, 512], F32, name="tr")
+            else:
+                acc = ps_mm.tile([P, 512], F32, name="mm")
             ms = slice(P * (m % 2), P * (m % 2) + P)
             nc.tensor.matmul_mx(
                 out=acc[:],
@@ -241,22 +255,29 @@ def tile_attention_prop_pa_kernel(tc, x_bytes, x_scale, w1, b1, w2, b2, gamma, b
                     out=junk[:], in_=src, func=ACT.Square, scale=1.0 / 32.0, accum_out=squares[m][:, h : h + 1]
                 )
 
+        def square_part(m):
+            nc.vector.tensor_scalar(
+                out=small[m][:, 3:4], in0=squares[m][:, 0:1], scalar1=EPS, scalar2=None, op0=ALU.add
+            )
+
+        def mean_part(m):
+            nc.vector.tensor_scalar(
+                out=small[m][:, 6:7],
+                in0=sums[m][:, 0:1],
+                scalar1=sums[m][:, 1:2],
+                scalar2=-1.0 / ROWS,
+                op0=ALU.add,
+                op1=ALU.mult,
+            )
+
         def aggregate(m):
             s = small[m]
             if m in BY_STATS:
                 nc.vector.bn_aggr(out=mv[m][:], in_=stats[m][:].rearrange("p a b -> p (a b)"))
             else:
-                nc.gpsimd.tensor_scalar(out=s[:, 3:4], in0=squares[m][:, 0:1], scalar1=EPS, scalar2=None, op0=ALU.add)
-                nc.gpsimd.tensor_scalar(
-                    out=s[:, 6:7],
-                    in0=sums[m][:, 0:1],
-                    scalar1=sums[m][:, 1:2],
-                    scalar2=-1.0 / ROWS,
-                    op0=ALU.add,
-                    op1=ALU.mult,
+                nc.vector.scalar_tensor_tensor(
+                    out=s[:, 4:5], in0=s[:, 6:7], scalar=s[:, 6:7], in1=s[:, 3:4], op0=ALU.mult, op1=ALU.subtract
                 )
-                nc.gpsimd.tensor_tensor(out=s[:, 5:6], in0=s[:, 6:7], in1=s[:, 6:7], op=ALU.mult)
-                nc.gpsimd.tensor_tensor(out=s[:, 4:5], in0=s[:, 3:4], in1=s[:, 5:6], op=ALU.subtract)
 
         def deviation(m):
             s = small[m]
@@ -265,7 +286,7 @@ def tile_attention_prop_pa_kernel(tc, x_bytes, x_scale, w1, b1, w2, b2, gamma, b
                 nc.scalar.activation(out=s[:, 6:7], in_=mv[m][:, 0:1], func=ACT.Identity, scale=-1.0)
             else:
                 nc.scalar.activation(
-                    out=s[:, 0:1], in_=squares[m][:, 1:2], func=ACT.Abs_reciprocal_sqrt, bias=s[:, 4:5]
+                    out=s[:, 0:1], in_=squares[m][:, 1:2], func=ACT.Abs_reciprocal_sqrt, scale=-1.0, bias=s[:, 4:5]
                 )
 
         def coeff_a(m):
@@ -291,143 +312,163 @@ def tile_attention_prop_pa_kernel(tc, x_bytes, x_scale, w1, b1, w2, b2, gamma, b
                     out=y[m][:, hs], in0=h2[m][:, hs], scalar1=s[:, 1:2], scalar2=s[:, 2:3], op0=ALU.mult, op1=ALU.add
                 )
 
-        def turn_y(m, h):
-            pt = ps_mm.tile([P, 4, P], F32, name="mm")
-            for b in range(4):
-                col = 512 * h + P * b
-                nc.tensor.transpose(pt[:, b, :], y[m][:, col : col + P], ident[:])
-            ps["y", m, h] = pt
-
-        def copy_y(m, h, eng):
-            o = stage.tile([P, 4, P], F32, name="o_sb", align_bytes=64)
-            if eng == "act":
-                nc.scalar.copy(out=o[:], in_=ps["y", m, h][:])
+        def turn_y(half, q):
+            if q % 2 == 0:
+                pt = ps_tr.tile([P, 2, 2, P], F32, name="tr")
             else:
-                nc.vector.tensor_copy(out=o[:], in_=ps["y", m, h][:])
-            nc.sync.dma_start(out=out_view[:, 4 * h : 4 * h + 4, P * m : P * m + P], in_=o[:])
+                pt = ps_mm.tile([P, 2, 2, P], F32, name="mm")
+            for b in range(2):
+                for i in range(2):
+                    col = P * (2 * q + b)
+                    nc.tensor.transpose(pt[:, b, i, :], y[2 * half + i][:, col : col + P], ident[:])
+            ps["y", half, q] = pt
 
-        widen(2, "act")
-        widen(0, "dve")
-        widen(1, "dve")
-        group_w1(0, "pool")
-        turn_x(0)
-        turn_x(1)
-        scale_x(0)
-        scale_x(1)
+        def copy_y(half, q, eng):
+            o = stage.tile([P, 2, 2 * P], F32, name="o_sb", align_bytes=64)
+            src = ps["y", half, q][:].rearrange("p b i c -> p b (i c)")
+            if eng == "act":
+                nc.scalar.copy(out=o[:], in_=src)
+            else:
+                nc.vector.tensor_copy(out=o[:], in_=src)
+            nc.sync.dma_start(out=out_view[:, 2 * q : 2 * q + 2, 2 * P * half : 2 * P * half + 2 * P], in_=o[:])
+
+        warm()
+        widen(0, 1, "act")
+        warm()
+        warm()
+        warm()
+        widen(1, 1, "dve")
+        turn_x(1, 1)
+        widen(2, 2, "dve")
+        widen(4, 2, "dve")
+        widen(6, 2, "act")
+        scale_x(1, 1)
+        group_w1(0, "act")
         group_w1(1, "act")
-        quant_w1(1)
-        turn_x(2)
-        widen(3, "act")
+        turn_x(2, 2)
+        scale_x(2, 2)
+        group_w2(1, "dve")
         turn_rows()
-        quant_x(1)
-        columns()
+        turn_x(0, 1)
+        turn_x(6, 2)
         group_w2(0, "act")
         group_w2(3, "act")
-        turn_x(3)
+        scale_x(0, 1)
+        turn_x(4, 2)
+        quant_x(1)
         quant_x(0)
-        quant_w1(0)
-        scale_x(2)
         group_w2(2, "act")
-        group_w2(1, "act")
-        scale_x(3)
-        mm1(0, 2)
-        mm1(0, 0)
-        bias1(0, 2)
-        mm1(0, 1)
-        quant_x(2)
-        quant_x(3)
+        quant_w1(1)
         mm1(0, 3)
-        mm1(1, 0)
-        bias1(0, 0)
-        quant_w2(1)
-        bias1(0, 1)
-        bounds()
         bias1(0, 3)
+        quant_w1(0)
+        scale_x(6, 2)
+        scale_x(4, 2)
         quant_w2(0)
+        mm1(0, 2)
+        bias1(0, 2)
+        columns()
+        quant_x(3)
+        mm1(0, 0)
+        bias1(0, 0)
+        quant_x(2)
+        bounds()
+        mm1(0, 1)
+        bias1(0, 1)
+        quant_w2(1)
+        mm1(1, 2)
         leaky1(0)
+        mm1(1, 1)
+        bias1(1, 1)
         mm1(1, 3)
         leaky1(1)
-        bias1(1, 0)
-        quant_h(0)
-        mm1(1, 2)
         bias1(1, 3)
-        bias1(1, 2)
-        mm1(1, 1)
+        quant_h(0)
+        mm1(1, 0)
         quant_h(1)
-        mm2(0, 0)
         mm2(1, 0)
-        mm2(3, 0)
-        bias1(1, 1)
-        leaky1(2)
+        bias1(1, 0)
+        bias1(1, 2)
         leaky1(3)
-        quant_h(2)
-        quant_h(3)
+        leaky1(2)
         low2(1, 0)
         mm2(2, 0)
-        low2(0, 0)
-        low2(3, 0)
         low2(2, 0)
-        leaky2(0, 0)
-        leaky2(3, 0)
-        leaky2(1, 0)
-        mm2(0, 1)
-        low2(0, 1)
-        mm2(1, 1)
-        leaky2(0, 1)
-        mm2(3, 1)
-        low2(1, 1)
-        mm2(2, 1)
-        stat(0, 0)
-        low2(3, 1)
-        stat(0, 1)
-        stat(1, 0)
-        aggregate(0)
+        quant_h(3)
+        quant_h(2)
         leaky2(2, 0)
-        deviation(0)
-        leaky2(1, 1)
-        leaky2(3, 1)
-        low2(2, 1)
+        mm2(3, 0)
+        low2(3, 0)
+        leaky2(3, 0)
+        mm2(0, 0)
+        low2(0, 0)
+        leaky2(0, 0)
         stat(3, 0)
-        coeff_a(0)
-        stat(1, 1)
+        mm2(3, 1)
         stat(2, 0)
-        aggregate(1)
-        deviation(1)
-        coeff_b(0)
+        square_part(2)
+        low2(3, 1)
+        leaky2(3, 1)
+        mm2(2, 1)
+        low2(2, 1)
         leaky2(2, 1)
-        norm(0, 0, "dve")
         stat(3, 1)
-        norm(0, 1, "act")
-        coeff_a(1)
+        mm2(1, 1)
+        low2(1, 1)
+        mm2(0, 1)
+        mean_part(2)
+        leaky2(1, 0)
+        low2(0, 1)
+        warm()
         aggregate(2)
-        turn_y(0, 0)
-        coeff_b(1)
         stat(2, 1)
-        aggregate(3)
-        norm(1, 1, "dve")
-        deviation(3)
-        norm(1, 0, "dve")
-        turn_y(0, 1)
+        stat(0, 0)
         deviation(2)
-        copy_y(0, 0, "act")
-        turn_y(1, 1)
-        coeff_a(2)
+        aggregate(3)
+        leaky2(0, 1)
+        deviation(3)
+        stat(1, 0)
         coeff_a(3)
-        turn_y(1, 0)
-        copy_y(0, 1, "act")
-        copy_y(1, 1, "act")
-        copy_y(1, 0, "act")
-        coeff_b(2)
+        coeff_a(2)
+        square_part(0)
+        mean_part(0)
+        stat(0, 1)
         coeff_b(3)
+        norm(3, 0, "act")
+        warm()
+        coeff_b(2)
+        leaky2(1, 1)
         norm(2, 0, "dve")
+        square_part(1)
+        aggregate(0)
+        stat(1, 1)
+        mean_part(1)
+        norm(3, 1, "dve")
+        deviation(0)
+        aggregate(1)
         norm(2, 1, "dve")
-        turn_y(2, 0)
-        norm(3, 0, "dve")
-        turn_y(2, 1)
-        norm(3, 1, "act")
-        turn_y(3, 0)
-        copy_y(2, 0, "dve")
-        copy_y(2, 1, "act")
-        copy_y(3, 0, "act")
-        turn_y(3, 1)
-        copy_y(3, 1, "act")
+        deviation(1)
+        turn_y(1, 0)
+        copy_y(1, 0, "act")
+        coeff_a(0)
+        coeff_a(1)
+        turn_y(1, 1)
+        copy_y(1, 1, "act")
+        coeff_b(0)
+        coeff_b(1)
+        norm(0, 1, "dve")
+        norm(1, 1, "dve")
+        turn_y(1, 2)
+        copy_y(1, 2, "dve")
+        turn_y(1, 3)
+        copy_y(1, 3, "act")
+        turn_y(0, 3)
+        turn_y(0, 2)
+        copy_y(0, 3, "act")
+        copy_y(0, 2, "act")
+        norm(1, 0, "dve")
+        norm(0, 0, "dve")
+        turn_y(0, 0)
+        copy_y(0, 0, "dve")
+        turn_y(0, 1)
+        copy_y(0, 1, "dve")

@@ -283,11 +283,19 @@ def tile_attention_prop_pa_kernel(tc, x_bytes, x_scale, w1, b1, w2, b2, gamma, b
             s = small[m]
             if m in BY_STATS:
                 nc.scalar.activation(out=s[:, 0:1], in_=mv[m][:, 1:2], func=ACT.Abs_reciprocal_sqrt, bias=EPS)
-                nc.scalar.activation(out=s[:, 6:7], in_=mv[m][:, 0:1], func=ACT.Identity, scale=-1.0)
             else:
                 nc.scalar.activation(
                     out=s[:, 0:1], in_=squares[m][:, 1:2], func=ACT.Abs_reciprocal_sqrt, scale=-1.0, bias=s[:, 4:5]
                 )
+
+        def mean_gamma(m):
+            s = small[m]
+            if m in BY_STATS:
+                nc.vector.scalar_tensor_tensor(
+                    out=s[:, 5:6], in0=mv[m][:, 0:1], scalar=-1.0, in1=cols[:, 4 + m : 5 + m], op0=ALU.mult, op1=ALU.mult
+                )
+            else:
+                nc.vector.tensor_tensor(out=s[:, 5:6], in0=s[:, 6:7], in1=cols[:, 4 + m : 5 + m], op=ALU.mult)
 
         def coeff_a(m):
             s = small[m]
@@ -296,7 +304,7 @@ def tile_attention_prop_pa_kernel(tc, x_bytes, x_scale, w1, b1, w2, b2, gamma, b
         def coeff_b(m):
             s = small[m]
             nc.vector.scalar_tensor_tensor(
-                out=s[:, 2:3], in0=s[:, 6:7], scalar=s[:, 1:2], in1=cols[:, 8 + m : 9 + m], op0=ALU.mult, op1=ALU.add
+                out=s[:, 2:3], in0=s[:, 0:1], scalar=s[:, 5:6], in1=cols[:, 8 + m : 9 + m], op0=ALU.mult, op1=ALU.add
             )
 
         def norm(m, h, eng):
@@ -332,143 +340,147 @@ def tile_attention_prop_pa_kernel(tc, x_bytes, x_scale, w1, b1, w2, b2, gamma, b
                 nc.vector.tensor_copy(out=o[:], in_=src)
             nc.sync.dma_start(out=out_view[:, 2 * q : 2 * q + 2, 2 * P * half : 2 * P * half + 2 * P], in_=o[:])
 
+        widen(1, 1, "dve")
         warm()
         widen(0, 1, "act")
         warm()
-        warm()
-        warm()
-        widen(1, 1, "dve")
         turn_x(1, 1)
+        widen(4, 2, "act")
         widen(2, 2, "dve")
-        widen(4, 2, "dve")
-        widen(6, 2, "act")
+        widen(6, 2, "dve")
         scale_x(1, 1)
-        group_w1(0, "act")
-        group_w1(1, "act")
         turn_x(2, 2)
         scale_x(2, 2)
         group_w2(1, "dve")
+        group_w1(0, "act")
+        group_w1(1, "act")
         turn_rows()
         turn_x(0, 1)
-        turn_x(6, 2)
-        group_w2(0, "act")
-        group_w2(3, "act")
         scale_x(0, 1)
-        turn_x(4, 2)
+        columns()
         quant_x(1)
         quant_x(0)
-        group_w2(2, "act")
-        quant_w1(1)
-        mm1(0, 3)
-        bias1(0, 3)
         quant_w1(0)
-        scale_x(6, 2)
+        quant_w1(1)
+        turn_x(4, 2)
+        group_w2(2, "act")
         scale_x(4, 2)
-        quant_w2(0)
-        mm1(0, 2)
-        bias1(0, 2)
-        columns()
-        quant_x(3)
-        mm1(0, 0)
-        bias1(0, 0)
+        turn_x(6, 2)
+        scale_x(6, 2)
+        group_w2(3, "act")
         quant_x(2)
-        bounds()
+        group_w2(0, "act")
         mm1(0, 1)
         bias1(0, 1)
-        quant_w2(1)
+        mm1(0, 2)
+        bias1(0, 2)
+        mm1(0, 3)
+        bias1(0, 3)
+        bounds()
+        mm1(0, 0)
+        bias1(0, 0)
+        quant_x(3)
+        mm1(1, 3)
+        bias1(1, 3)
+        mm1(1, 0)
         mm1(1, 2)
-        leaky1(0)
+        bias1(1, 2)
+        bias1(1, 0)
+        quant_w2(1)
         mm1(1, 1)
         bias1(1, 1)
-        mm1(1, 3)
+        quant_w2(0)
+        leaky1(0)
         leaky1(1)
-        bias1(1, 3)
         quant_h(0)
-        mm1(1, 0)
         quant_h(1)
-        mm2(1, 0)
-        bias1(1, 0)
-        bias1(1, 2)
-        leaky1(3)
-        leaky1(2)
-        low2(1, 0)
-        mm2(2, 0)
-        low2(2, 0)
-        quant_h(3)
-        quant_h(2)
-        leaky2(2, 0)
         mm2(3, 0)
-        low2(3, 0)
-        leaky2(3, 0)
+        mm2(1, 0)
+        mm2(2, 0)
+        leaky1(2)
+        leaky1(3)
+        quant_h(2)
         mm2(0, 0)
-        low2(0, 0)
-        leaky2(0, 0)
-        stat(3, 0)
-        mm2(3, 1)
-        stat(2, 0)
-        square_part(2)
-        low2(3, 1)
-        leaky2(3, 1)
+        quant_h(3)
+        low2(3, 0)
+        mm2(0, 1)
         mm2(2, 1)
-        low2(2, 1)
-        leaky2(2, 1)
-        stat(3, 1)
+        low2(1, 0)
+        leaky2(1, 0)
+        low2(2, 0)
+        leaky2(2, 0)
+        low2(0, 0)
+        stat(1, 0)
+        leaky2(0, 0)
+        leaky2(3, 0)
+        low2(0, 1)
+        leaky2(0, 1)
         mm2(1, 1)
         low2(1, 1)
-        mm2(0, 1)
-        mean_part(2)
-        leaky2(1, 0)
-        low2(0, 1)
-        warm()
-        aggregate(2)
-        stat(2, 1)
-        stat(0, 0)
-        deviation(2)
-        aggregate(3)
-        leaky2(0, 1)
-        deviation(3)
-        stat(1, 0)
-        coeff_a(3)
-        coeff_a(2)
-        square_part(0)
-        mean_part(0)
-        stat(0, 1)
-        coeff_b(3)
-        norm(3, 0, "act")
-        warm()
-        coeff_b(2)
         leaky2(1, 1)
-        norm(2, 0, "dve")
+        stat(0, 0)
+        warm()
+        low2(2, 1)
+        mean_part(0)
+        warm()
+        warm()
+        square_part(0)
         square_part(1)
+        mean_part(1)
+        mean_gamma(0)
+        stat(0, 1)
         aggregate(0)
         stat(1, 1)
-        mean_part(1)
-        norm(3, 1, "dve")
         deviation(0)
+        stat(3, 0)
         aggregate(1)
-        norm(2, 1, "dve")
+        leaky2(2, 1)
+        mean_gamma(1)
         deviation(1)
+        coeff_b(0)
+        mm2(3, 1)
+        warm()
+        low2(3, 1)
+        stat(2, 0)
+        coeff_a(0)
+        stat(2, 1)
+        mean_part(2)
+        coeff_b(1)
+        coeff_a(1)
+        norm(0, 0, "dve")
+        norm(1, 0, "dve")
+        norm(0, 1, "act")
+        leaky2(3, 1)
+        square_part(2)
+        norm(1, 1, "dve")
+        turn_y(0, 1)
+        copy_y(0, 1, "act")
+        stat(3, 1)
+        mean_gamma(2)
+        aggregate(2)
+        deviation(2)
+        aggregate(3)
+        deviation(3)
+        mean_gamma(3)
+        coeff_b(2)
+        turn_y(0, 0)
+        coeff_a(2)
+        copy_y(0, 0, "act")
+        coeff_b(3)
+        coeff_a(3)
+        turn_y(0, 3)
+        norm(2, 0, "dve")
+        copy_y(0, 3, "act")
+        turn_y(0, 2)
+        copy_y(0, 2, "act")
+        norm(3, 0, "dve")
         turn_y(1, 0)
         copy_y(1, 0, "act")
-        coeff_a(0)
-        coeff_a(1)
+        norm(2, 1, "dve")
+        norm(3, 1, "dve")
         turn_y(1, 1)
-        copy_y(1, 1, "act")
-        coeff_b(0)
-        coeff_b(1)
-        norm(0, 1, "dve")
-        norm(1, 1, "dve")
-        turn_y(1, 2)
-        copy_y(1, 2, "dve")
+        copy_y(1, 1, "dve")
         turn_y(1, 3)
         copy_y(1, 3, "act")
-        turn_y(0, 3)
-        turn_y(0, 2)
-        copy_y(0, 3, "act")
-        copy_y(0, 2, "act")
-        norm(1, 0, "dve")
-        norm(0, 0, "dve")
-        turn_y(0, 0)
-        copy_y(0, 0, "dve")
-        turn_y(0, 1)
-        copy_y(0, 1, "dve")
+        turn_y(1, 2)
+        copy_y(1, 2, "dve")

@@ -91,6 +91,7 @@ def tile_attention_prop_pa_kernel(tc, x_bytes, x_scale, w1, b1, w2, b2, gamma, b
         xg = {}
         v1 = [keep.tile([P, 4, 512], F32, name="v1_%d" % h, align_bytes=64) for h in range(2)]
         hg = {}
+        hf = {}
         u2 = {}
 
         def warm():
@@ -206,6 +207,22 @@ def tile_attention_prop_pa_kernel(tc, x_bytes, x_scale, w1, b1, w2, b2, gamma, b
             nc.vector.scalar_tensor_tensor(
                 out=g[:].rearrange("p (n t) -> p n t", t=4), in0=v, scalar=SLOPE, in1=v, op0=ALU.mult, op1=ALU.max
             )
+            hg[c] = g
+
+        def leaky1_flat(c):
+            f = work.tile([P, 4, 256], BF16, name="h_f", align_bytes=64)
+            v = v1[c // 2][:, :, 256 * (c % 2) : 256 * (c % 2) + 256]
+            nc.vector.scalar_tensor_tensor(out=f[:], in0=v, scalar=SLOPE, in1=v, op0=ALU.mult, op1=ALU.max)
+            hf[c] = f
+
+        def group_h(c, eng):
+            g = work.tile([P, 1024], BF16, name="h_g", align_bytes=64)
+            dst = g[:].rearrange("p (k i t) -> p k t i", i=4, t=4)
+            src = hf[c][:].rearrange("p t (k i) -> p k t i", i=4)
+            if eng == "act":
+                nc.scalar.copy(out=dst, in_=src)
+            else:
+                nc.vector.tensor_copy(out=dst, in_=src)
             hg[c] = g
 
         def quant_h(c):
@@ -340,147 +357,145 @@ def tile_attention_prop_pa_kernel(tc, x_bytes, x_scale, w1, b1, w2, b2, gamma, b
                 nc.vector.tensor_copy(out=o[:], in_=src)
             nc.sync.dma_start(out=out_view[:, 2 * q : 2 * q + 2, 2 * P * half : 2 * P * half + 2 * P], in_=o[:])
 
-        widen(1, 1, "dve")
         warm()
-        widen(0, 1, "act")
         warm()
-        turn_x(1, 1)
-        widen(4, 2, "act")
+        widen(0, 1, "dve")
+        widen(1, 1, "act")
+        widen(6, 2, "act")
         widen(2, 2, "dve")
-        widen(6, 2, "dve")
-        scale_x(1, 1)
-        turn_x(2, 2)
-        scale_x(2, 2)
-        group_w2(1, "dve")
-        group_w1(0, "act")
-        group_w1(1, "act")
-        turn_rows()
+        widen(4, 2, "dve")
         turn_x(0, 1)
         scale_x(0, 1)
-        columns()
+        turn_x(2, 2)
+        scale_x(2, 2)
+        group_w1(0, "act")
+        quant_w1(0)
+        group_w1(1, "act")
+        turn_x(1, 1)
+        scale_x(1, 1)
+        group_w2(3, "act")
+        group_w2(1, "act")
+        turn_rows()
+        group_w2(0, "act")
         quant_x(1)
         quant_x(0)
-        quant_w1(0)
+        turn_x(6, 2)
         quant_w1(1)
         turn_x(4, 2)
-        group_w2(2, "act")
-        scale_x(4, 2)
-        turn_x(6, 2)
+        mm1(0, 0)
         scale_x(6, 2)
-        group_w2(3, "act")
-        quant_x(2)
-        group_w2(0, "act")
+        bias1(0, 0)
+        scale_x(4, 2)
         mm1(0, 1)
         bias1(0, 1)
-        mm1(0, 2)
-        bias1(0, 2)
         mm1(0, 3)
         bias1(0, 3)
-        bounds()
-        mm1(0, 0)
-        bias1(0, 0)
+        mm1(0, 2)
         quant_x(3)
-        mm1(1, 3)
-        bias1(1, 3)
-        mm1(1, 0)
+        quant_x(2)
+        columns()
+        bias1(0, 2)
         mm1(1, 2)
         bias1(1, 2)
-        bias1(1, 0)
+        group_w2(2, "dve")
+        quant_w2(0)
         quant_w2(1)
         mm1(1, 1)
         bias1(1, 1)
-        quant_w2(0)
-        leaky1(0)
+        bounds()
+        leaky1_flat(0)
+        mm1(1, 0)
         leaky1(1)
-        quant_h(0)
+        mm1(1, 3)
+        bias1(1, 0)
+        bias1(1, 3)
+        leaky1_flat(2)
         quant_h(1)
+        group_h(0, "act")
+        quant_h(0)
         mm2(3, 0)
-        mm2(1, 0)
-        mm2(2, 0)
-        leaky1(2)
         leaky1(3)
+        group_h(2, "act")
         quant_h(2)
-        mm2(0, 0)
+        mm2(2, 0)
         quant_h(3)
         low2(3, 0)
-        mm2(0, 1)
-        mm2(2, 1)
-        low2(1, 0)
-        leaky2(1, 0)
+        leaky2(3, 0)
+        mm2(1, 0)
         low2(2, 0)
         leaky2(2, 0)
+        stat(3, 0)
+        low2(1, 0)
+        leaky2(1, 0)
+        mm2(0, 0)
         low2(0, 0)
-        stat(1, 0)
-        leaky2(0, 0)
-        leaky2(3, 0)
-        low2(0, 1)
-        leaky2(0, 1)
+        mm2(3, 1)
+        low2(3, 1)
+        leaky2(3, 1)
+        mm2(2, 1)
+        low2(2, 1)
+        leaky2(2, 1)
+        stat(3, 1)
+        mean_part(2)
         mm2(1, 1)
         low2(1, 1)
-        leaky2(1, 1)
-        stat(0, 0)
-        warm()
-        low2(2, 1)
-        mean_part(0)
-        warm()
-        warm()
-        square_part(0)
-        square_part(1)
-        mean_part(1)
-        mean_gamma(0)
-        stat(0, 1)
-        aggregate(0)
-        stat(1, 1)
-        deviation(0)
-        stat(3, 0)
-        aggregate(1)
-        leaky2(2, 1)
-        mean_gamma(1)
-        deviation(1)
-        coeff_b(0)
-        mm2(3, 1)
-        warm()
-        low2(3, 1)
         stat(2, 0)
-        coeff_a(0)
-        stat(2, 1)
-        mean_part(2)
-        coeff_b(1)
-        coeff_a(1)
-        norm(0, 0, "dve")
-        norm(1, 0, "dve")
-        norm(0, 1, "act")
-        leaky2(3, 1)
         square_part(2)
-        norm(1, 1, "dve")
-        turn_y(0, 1)
-        copy_y(0, 1, "act")
-        stat(3, 1)
-        mean_gamma(2)
-        aggregate(2)
-        deviation(2)
         aggregate(3)
-        deviation(3)
+        aggregate(2)
+        mean_gamma(2)
+        stat(2, 1)
+        leaky2(1, 1)
+        mm2(0, 1)
         mean_gamma(3)
+        stat(1, 0)
+        deviation(2)
         coeff_b(2)
-        turn_y(0, 0)
         coeff_a(2)
-        copy_y(0, 0, "act")
-        coeff_b(3)
+        square_part(1)
+        deviation(3)
         coeff_a(3)
-        turn_y(0, 3)
-        norm(2, 0, "dve")
-        copy_y(0, 3, "act")
-        turn_y(0, 2)
-        copy_y(0, 2, "act")
+        mean_part(1)
+        coeff_b(3)
+        leaky2(0, 0)
+        aggregate(1)
+        low2(0, 1)
         norm(3, 0, "dve")
+        leaky2(0, 1)
+        norm(2, 1, "dve")
+        norm(2, 0, "act")
+        mean_gamma(1)
+        mean_part(0)
+        stat(1, 1)
+        stat(0, 0)
+        square_part(0)
+        norm(3, 1, "dve")
+        deviation(1)
+        coeff_b(1)
+        aggregate(0)
+        stat(0, 1)
+        deviation(0)
+        coeff_a(1)
+        turn_y(1, 1)
+        mean_gamma(0)
+        copy_y(1, 1, "dve")
         turn_y(1, 0)
         copy_y(1, 0, "act")
-        norm(2, 1, "dve")
-        norm(3, 1, "dve")
-        turn_y(1, 1)
-        copy_y(1, 1, "dve")
+        coeff_b(0)
+        turn_y(1, 2)
+        copy_y(1, 2, "act")
+        coeff_a(0)
+        norm(1, 0, "dve")
         turn_y(1, 3)
         copy_y(1, 3, "act")
-        turn_y(1, 2)
-        copy_y(1, 2, "dve")
+        norm(0, 0, "dve")
+        turn_y(0, 1)
+        copy_y(0, 1, "act")
+        norm(1, 1, "dve")
+        norm(0, 1, "dve")
+        turn_y(0, 3)
+        copy_y(0, 3, "act")
+        turn_y(0, 2)
+        copy_y(0, 2, "dve")
+        turn_y(0, 0)
+        copy_y(0, 0, "dve")

from contextlib import ExitStack

import concourse.mybir as mybir
from concourse.masks import make_identity

F32 = mybir.dt.float32
BF16 = mybir.dt.bfloat16
U32 = mybir.dt.uint32
U8 = mybir.dt.uint8
FP8 = mybir.dt.float8_e4m3fn
FP8X4 = mybir.dt.float8_e4m3fn_x4
ALU = mybir.AluOpType
ACT = mybir.ActivationFunctionType

P = 128
ROWS = 1024
K = 512
CH = 512
NB = 8
SLOPE = 0.01
EPS = 1e-5
BY_STATS = (3,)
FLOPS = 2 * 2 * ROWS * K * CH


def tile_attention_prop_pa_kernel(tc, x_bytes, x_scale, w1, b1, w2, b2, gamma, beta, out):
    nc = tc.nc
    with ExitStack() as ctx:
        keep = ctx.enter_context(tc.tile_pool(name="keep", bufs=1))
        work = ctx.enter_context(tc.tile_pool(name="work", bufs=4))
        stage = ctx.enter_context(tc.tile_pool(name="stage", bufs=8))
        ps_tr = ctx.enter_context(tc.psum_pool(name="ps_tr", bufs=2))
        ps_mm = ctx.enter_context(tc.psum_pool(name="ps_mm", bufs=6))
        ctx.enter_context(tc.manual_schedule())

        sc4 = keep.tile([P, 4], F32, name="sc4")
        x_first = [keep.tile([P, 2, K], U8, name="x_first%d" % c, align_bytes=64) for c in range(2)]
        x_rest = keep.tile([P, 4, K], U8, name="x_rest", align_bytes=64)
        w1_raw = keep.tile([P, 4, CH], BF16, name="w1_raw", align_bytes=64)
        w2_raw = keep.tile([P, 4, CH], BF16, name="w2_raw", align_bytes=64)
        w1_grp = [keep.tile([P, 1024], BF16, name="w1_grp%d" % i, align_bytes=64) for i in range(2)]
        w2_grp = [keep.tile([P, 1024], BF16, name="w2_grp%d" % i, align_bytes=64) for i in range(2)]
        w1_q = [keep.tile([P, 256], U32, name="w1_q%d" % i, align_bytes=64) for i in range(2)]
        w2_q = [keep.tile([P, 256], U32, name="w2_q%d" % i, align_bytes=64) for i in range(2)]
        w1_s = [keep.tile([P, 256], U8, name="w1_s%d" % i, align_bytes=64) for i in range(2)]
        w2_s = [keep.tile([P, 256], U8, name="w2_s%d" % i, align_bytes=64) for i in range(2)]
        x_q = [keep.tile([P, 512], U32, name="x_q%d" % i, align_bytes=64) for i in range(2)]
        x_s = [keep.tile([P, 512], U8, name="x_s%d" % i, align_bytes=64) for i in range(2)]
        h_q = [keep.tile([P, 512], U32, name="h_q%d" % i, align_bytes=64) for i in range(2)]
        h_s = [keep.tile([P, 512], U8, name="h_s%d" % i, align_bytes=64) for i in range(2)]
        h2 = [keep.tile([P, ROWS], F32, name="h2_%d" % m, align_bytes=64) for m in range(4)]
        y = [keep.tile([P, ROWS], F32, name="y_%d" % m, align_bytes=64) for m in range(4)]
        stats = [keep.tile([P, 2, 6], F32, name="stats%d" % m) for m in range(4)]
        mv = [keep.tile([P, 2], F32, name="mv%d" % m) for m in range(4)]
        small = [keep.tile([P, 8], F32, name="small%d" % m) for m in range(4)]
        b1_c = keep.tile([P, 4], BF16, name="b1_c")
        rows = keep.tile([P, P], BF16, name="rows")
        cols = keep.tile([P, 12], F32, name="cols")
        b_hi = keep.tile([P, 4], F32, name="b_hi")
        b_lo = keep.tile([P, 4], F32, name="b_lo")
        sums = [keep.tile([P, 2], F32, name="sums%d" % m) for m in range(4)]
        squares = [keep.tile([P, 2], F32, name="squares%d" % m) for m in range(4)]
        ident = keep.tile([P, P], F32, name="ident")
        ident_b = keep.tile([P, P], BF16, name="ident_b")
        zeros = keep.tile([P, 512], BF16, name="zeros", align_bytes=64)
        half = keep.tile([P, 1], F32, name="half")
        dummy = keep.tile([P, 1], F32, name="dummy")

        x_view = x_bytes.rearrange("(p b) k -> p b k", b=NB)
        out_view = out.rearrange("(p b) c -> p b c", b=NB)

        nc.sync.dma_start(out=x_first[0][:], in_=x_view[:, 0:2, :])
        nc.sync.dma_start(out=sc4[:], in_=x_scale.rearrange("o (p t) -> p (o t)", t=4))
        nc.sync.dma_start(out=x_first[1][:], in_=x_view[:, 2:4, :])
        nc.sync.dma_start(out=x_rest[:], in_=x_view[:, 4:8, :])
        nc.vector.memset(zeros[:], 0.0)
        nc.vector.memset(rows[:], 0.0)
        nc.vector.memset(half[:], 1.0)
        nc.scalar.dma_start(out=b1_c[:], in_=b1.rearrange("(p t) -> p t", t=4))
        nc.scalar.activation(out=dummy[:], in_=half[:], func=ACT.Abs_reciprocal_sqrt)
        nc.sync.dma_start(out=w1_raw[:], in_=w1.rearrange("(p j) c -> p j c", j=4))
        nc.scalar.dma_start(out=rows[0:4, :], in_=b2.rearrange("(m p) -> m p", p=P))
        nc.scalar.dma_start(out=rows[4:8, :], in_=gamma.rearrange("(m p) -> m p", p=P))
        nc.scalar.dma_start(out=rows[8:12, :], in_=beta.rearrange("(m p) -> m p", p=P))
        nc.sync.dma_start(out=w2_raw[:], in_=w2.rearrange("(p j) c -> p j c", j=4))
        make_identity(nc, ident[:])
        nc.vector.tensor_copy(out=ident_b[:], in_=ident[:])

        xw = {}
        ps = {}
        xg = {}
        v1 = [keep.tile([P, 4, 512], F32, name="v1_%d" % h, align_bytes=64) for h in range(2)]
        hg = {}
        hf = {}
        u2 = {}

        def warm():
            acc = ps_mm.tile([P, 512], F32, name="mm")
            nc.tensor.matmul(acc[:], lhsT=zeros[:, 0:P], rhs=zeros[:], start=True, stop=True)

        def widen(b, n, eng):
            t = work.tile([P, n * K], BF16, name="x_w%d" % n, align_bytes=64)
            src, b0 = (x_first[b // 2], b % 2) if b < 4 else (x_rest, b - 4)
            src = src[:, b0 : b0 + n, :].rearrange("p b k -> p (b k)").bitcast(FP8)
            if eng == "act":
                nc.scalar.copy(out=t[:], in_=src)
            elif eng == "dve":
                nc.vector.tensor_copy(out=t[:], in_=src)
            else:
                for i in range(n):
                    cs = slice(K * i, K * i + K)
                    nc.gpsimd.tensor_copy(out=t[:, cs], in_=src[:, cs])
            xw[b] = t

        def turn_x(b, n):
            pt = ps_tr.tile([P, 2, P * n], F32, name="tr")
            words = xw[b][:].bitcast(F32)
            for i in range(n):
                for u in range(2):
                    nc.tensor.transpose(
                        pt[:, u, P * i : P * i + P], words[:, 256 * i + u : 256 * i + 256 : 2], ident[:]
                    )
            ps["x", b] = pt

        def scale_x(b, n):
            c = b // 2
            if c not in xg:
                xg[c] = work.tile([P, 1024], BF16, name="x_g", align_bytes=64)
            r0 = 512 * (b % 2)
            nc.vector.tensor_tensor(
                out=xg[c][:, r0 : r0 + 512 * n].rearrange("p (r u e) -> p r u e", u=2, e=2),
                in0=ps["x", b][:].bitcast(BF16).rearrange("p u (r e) -> p r u e", e=2),
                in1=sc4[:].rearrange("p (o u e) -> p o u e", o=1, u=2).to_broadcast([P, P * n, 2, 2]),
                op=ALU.mult,
            )

        def quant_x(c):
            cs = slice(256 * (c % 2), 256 * (c % 2) + 256)
            nc.vector.quantize_mx(out=x_q[c // 2][:, cs].bitcast(FP8X4), scales=x_s[c // 2][:, cs], in_=xg[c][:])

        def group_w1(i, eng):
            dst = w1_grp[i][:].rearrange("p (t m j) -> p t m j", t=2, j=4)
            src = w1_raw[:].rearrange("p j (m t) -> p t m j", t=4)[:, 2 * i : 2 * i + 2, :, :]
            if eng == "act":
                nc.scalar.copy(out=dst, in_=src)
            elif eng == "dve":
                nc.vector.tensor_copy(out=dst, in_=src)
            else:
                for t in range(2):
                    nc.gpsimd.tensor_scalar(
                        out=dst[:, t, :, :], in0=src[:, t, :, :], scalar1=1.0, scalar2=0.0, op0=ALU.mult, op1=ALU.add
                    )

        def quant_w1(i):
            nc.vector.quantize_mx(out=w1_q[i][:].bitcast(FP8X4), scales=w1_s[i][:], in_=w1_grp[i][:])

        def group_w2(q, eng):
            dst = w2_grp[q // 2][:, 512 * (q % 2) : 512 * (q % 2) + 512].rearrange("p (c i j) -> p c j i", i=4, j=4)
            src = w2_raw[:, :, P * q : P * q + P].rearrange("p j (c i) -> p c j i", i=4)
            if eng == "act":
                nc.scalar.copy(out=dst, in_=src)
            elif eng == "dve":
                nc.vector.tensor_copy(out=dst, in_=src)
            else:
                nc.gpsimd.tensor_scalar(out=dst, in0=src, scalar1=1.0, scalar2=0.0, op0=ALU.mult, op1=ALU.add)

        def quant_w2(i):
            nc.vector.quantize_mx(out=w2_q[i][:].bitcast(FP8X4), scales=w2_s[i][:], in_=w2_grp[i][:])

        def turn_rows():
            ps["rows"] = ps_mm.tile([P, P], BF16, name="mm")
            nc.tensor.transpose(ps["rows"][:], rows[:], ident_b[:])

        def columns():
            nc.vector.tensor_copy(out=cols[:], in_=ps["rows"][:, 0:12])

        def bounds():
            nc.vector.tensor_scalar(
                out=b_hi[:], in0=cols[:, 0:4], scalar1=1.0 - SLOPE, scalar2=0.0, op0=ALU.mult, op1=ALU.min
            )
            nc.vector.tensor_scalar(
                out=b_lo[:], in0=cols[:, 0:4], scalar1=SLOPE - 1.0, scalar2=0.0, op0=ALU.mult, op1=ALU.min
            )

        def mm1(h, t):
            acc = ps_mm.tile([P, 512], F32, name="mm")
            ts = slice(P * (t % 2), P * (t % 2) + P)
            nc.tensor.matmul_mx(
                out=acc[:],
                lhsT=w1_q[t // 2][:, ts].bitcast(FP8X4),
                lhsT_scale=w1_s[t // 2][:, ts],
                rhs=x_q[h][:].bitcast(FP8X4),
                rhs_scale=x_s[h][:],
                start=True,
                stop=True,
            )
            ps["h", h, t] = acc

        def bias1(h, t):
            nc.scalar.activation(
                out=v1[h][:, t, :], in_=ps["h", h, t][:], func=ACT.Identity, bias=b1_c[:, t : t + 1]
            )

        def leaky1(c):
            g = work.tile([P, 1024], BF16, name="h_g", align_bytes=64)
            v = v1[c // 2][:, :, 256 * (c % 2) : 256 * (c % 2) + 256].rearrange("p t n -> p n t")
            nc.vector.scalar_tensor_tensor(
                out=g[:].rearrange("p (n t) -> p n t", t=4), in0=v, scalar=SLOPE, in1=v, op0=ALU.mult, op1=ALU.max
            )
            hg[c] = g

        def leaky1_flat(c):
            f = work.tile([P, 4, 256], BF16, name="h_f", align_bytes=64)
            v = v1[c // 2][:, :, 256 * (c % 2) : 256 * (c % 2) + 256]
            nc.vector.scalar_tensor_tensor(out=f[:], in0=v, scalar=SLOPE, in1=v, op0=ALU.mult, op1=ALU.max)
            hf[c] = f

        def group_h(c, eng):
            g = work.tile([P, 1024], BF16, name="h_g", align_bytes=64)
            dst = g[:].rearrange("p (k i t) -> p k t i", i=4, t=4)
            src = hf[c][:].rearrange("p t (k i) -> p k t i", i=4)
            if eng == "act":
                nc.scalar.copy(out=dst, in_=src)
            else:
                nc.vector.tensor_copy(out=dst, in_=src)
            hg[c] = g

        def quant_h(c):
            cs = slice(256 * (c % 2), 256 * (c % 2) + 256)
            nc.vector.quantize_mx(out=h_q[c // 2][:, cs].bitcast(FP8X4), scales=h_s[c // 2][:, cs], in_=hg[c][:])

        def mm2(m, h):
            if h == 1 and m >= 2:
                acc = ps_tr.tile([P, 512], F32, name="tr")
            else:
                acc = ps_mm.tile([P, 512], F32, name="mm")
            ms = slice(P * (m % 2), P * (m % 2) + P)
            nc.tensor.matmul_mx(
                out=acc[:],
                lhsT=w2_q[m // 2][:, ms].bitcast(FP8X4),
                lhsT_scale=w2_s[m // 2][:, ms],
                rhs=h_q[h][:].bitcast(FP8X4),
                rhs_scale=h_s[h][:],
                start=True,
                stop=True,
            )
            ps[m, h] = acc

        def low2(m, h):
            u = stage.tile([P, 512], F32, name="u2", align_bytes=64)
            nc.scalar.activation(out=u[:], in_=ps[m, h][:], func=ACT.Identity, bias=b_lo[:, m : m + 1], scale=SLOPE)
            u2[m, h] = u

        def leaky2(m, h):
            nc.vector.scalar_tensor_tensor(
                out=h2[m][:, 512 * h : 512 * h + 512],
                in0=ps[m, h][:],
                scalar=b_hi[:, m : m + 1],
                in1=u2[m, h][:],
                op0=ALU.add,
                op1=ALU.max,
                accum_out=None if m in BY_STATS else sums[m][:, h : h + 1],
            )

        def stat(m, h):
            src = h2[m][:, 512 * h : 512 * h + 512]
            if m in BY_STATS:
                nc.vector.bn_stats(out=stats[m][:, h, :], in_=src)
            else:
                junk = work.tile([P, 512], F32, name="junk", align_bytes=64)
                nc.scalar.activation(
                    out=junk[:], in_=src, func=ACT.Square, scale=1.0 / 32.0, accum_out=squares[m][:, h : h + 1]
                )

        def square_part(m):
            nc.vector.tensor_scalar(
                out=small[m][:, 3:4], in0=squares[m][:, 0:1], scalar1=EPS, scalar2=None, op0=ALU.add
            )

        def mean_part(m):
            nc.vector.tensor_scalar(
                out=small[m][:, 6:7],
                in0=sums[m][:, 0:1],
                scalar1=sums[m][:, 1:2],
                scalar2=-1.0 / ROWS,
                op0=ALU.add,
                op1=ALU.mult,
            )

        def aggregate(m):
            s = small[m]
            if m in BY_STATS:
                nc.vector.bn_aggr(out=mv[m][:], in_=stats[m][:].rearrange("p a b -> p (a b)"))
            else:
                nc.vector.scalar_tensor_tensor(
                    out=s[:, 4:5], in0=s[:, 6:7], scalar=s[:, 6:7], in1=s[:, 3:4], op0=ALU.mult, op1=ALU.subtract
                )

        def deviation(m):
            s = small[m]
            if m in BY_STATS:
                nc.scalar.activation(out=s[:, 0:1], in_=mv[m][:, 1:2], func=ACT.Abs_reciprocal_sqrt, bias=EPS)
            else:
                nc.scalar.activation(
                    out=s[:, 0:1], in_=squares[m][:, 1:2], func=ACT.Abs_reciprocal_sqrt, scale=-1.0, bias=s[:, 4:5]
                )

        def mean_gamma(m):
            s = small[m]
            if m in BY_STATS:
                nc.vector.scalar_tensor_tensor(
                    out=s[:, 5:6], in0=mv[m][:, 0:1], scalar=-1.0, in1=cols[:, 4 + m : 5 + m], op0=ALU.mult, op1=ALU.mult
                )
            else:
                nc.vector.tensor_tensor(out=s[:, 5:6], in0=s[:, 6:7], in1=cols[:, 4 + m : 5 + m], op=ALU.mult)

        def coeff_a(m):
            s = small[m]
            nc.vector.tensor_tensor(out=s[:, 1:2], in0=s[:, 0:1], in1=cols[:, 4 + m : 5 + m], op=ALU.mult)

        def coeff_b(m):
            s = small[m]
            nc.vector.scalar_tensor_tensor(
                out=s[:, 2:3], in0=s[:, 0:1], scalar=s[:, 5:6], in1=cols[:, 8 + m : 9 + m], op0=ALU.mult, op1=ALU.add
            )

        def norm(m, h, eng):
            hs = slice(512 * h, 512 * h + 512)
            s = small[m]
            if eng == "act":
                nc.scalar.activation(
                    out=y[m][:, hs], in_=h2[m][:, hs], func=ACT.Identity, bias=s[:, 2:3], scale=s[:, 1:2]
                )
            else:
                e = nc.gpsimd if eng == "pool" else nc.vector
                e.tensor_scalar(
                    out=y[m][:, hs], in0=h2[m][:, hs], scalar1=s[:, 1:2], scalar2=s[:, 2:3], op0=ALU.mult, op1=ALU.add
                )

        def turn_y(half, q):
            if q % 2 == 0:
                pt = ps_tr.tile([P, 2, 2, P], F32, name="tr")
            else:
                pt = ps_mm.tile([P, 2, 2, P], F32, name="mm")
            for b in range(2):
                for i in range(2):
                    col = P * (2 * q + b)
                    nc.tensor.transpose(pt[:, b, i, :], y[2 * half + i][:, col : col + P], ident[:])
            ps["y", half, q] = pt

        def copy_y(half, q, eng):
            o = stage.tile([P, 2, 2 * P], F32, name="o_sb", align_bytes=64)
            src = ps["y", half, q][:].rearrange("p b i c -> p b (i c)")
            if eng == "act":
                nc.scalar.copy(out=o[:], in_=src)
            else:
                nc.vector.tensor_copy(out=o[:], in_=src)
            nc.sync.dma_start(out=out_view[:, 2 * q : 2 * q + 2, 2 * P * half : 2 * P * half + 2 * P], in_=o[:])

        warm()
        warm()
        widen(0, 1, "dve")
        widen(1, 1, "act")
        widen(6, 2, "act")
        widen(2, 2, "dve")
        widen(4, 2, "dve")
        turn_x(0, 1)
        scale_x(0, 1)
        turn_x(2, 2)
        scale_x(2, 2)
        group_w1(0, "act")
        quant_w1(0)
        group_w1(1, "act")
        turn_x(1, 1)
        scale_x(1, 1)
        group_w2(3, "act")
        group_w2(1, "act")
        turn_rows()
        group_w2(0, "act")
        quant_x(1)
        quant_x(0)
        turn_x(6, 2)
        quant_w1(1)
        turn_x(4, 2)
        mm1(0, 0)
        scale_x(6, 2)
        bias1(0, 0)
        scale_x(4, 2)
        mm1(0, 1)
        bias1(0, 1)
        mm1(0, 3)
        bias1(0, 3)
        mm1(0, 2)
        quant_x(3)
        quant_x(2)
        columns()
        bias1(0, 2)
        mm1(1, 2)
        bias1(1, 2)
        group_w2(2, "dve")
        quant_w2(0)
        quant_w2(1)
        mm1(1, 1)
        bias1(1, 1)
        bounds()
        leaky1_flat(0)
        mm1(1, 0)
        leaky1(1)
        mm1(1, 3)
        bias1(1, 0)
        bias1(1, 3)
        leaky1_flat(2)
        quant_h(1)
        group_h(0, "act")
        quant_h(0)
        mm2(3, 0)
        leaky1(3)
        group_h(2, "act")
        quant_h(2)
        mm2(2, 0)
        quant_h(3)
        low2(3, 0)
        leaky2(3, 0)
        mm2(1, 0)
        low2(2, 0)
        leaky2(2, 0)
        stat(3, 0)
        low2(1, 0)
        leaky2(1, 0)
        mm2(0, 0)
        low2(0, 0)
        mm2(3, 1)
        low2(3, 1)
        leaky2(3, 1)
        mm2(2, 1)
        low2(2, 1)
        leaky2(2, 1)
        stat(3, 1)
        mean_part(2)
        mm2(1, 1)
        low2(1, 1)
        stat(2, 0)
        square_part(2)
        aggregate(3)
        aggregate(2)
        mean_gamma(2)
        stat(2, 1)
        leaky2(1, 1)
        mm2(0, 1)
        mean_gamma(3)
        stat(1, 0)
        deviation(2)
        coeff_b(2)
        coeff_a(2)
        square_part(1)
        deviation(3)
        coeff_a(3)
        mean_part(1)
        coeff_b(3)
        leaky2(0, 0)
        aggregate(1)
        low2(0, 1)
        norm(3, 0, "dve")
        leaky2(0, 1)
        norm(2, 1, "dve")
        norm(2, 0, "act")
        mean_gamma(1)
        mean_part(0)
        stat(1, 1)
        stat(0, 0)
        square_part(0)
        norm(3, 1, "dve")
        deviation(1)
        coeff_b(1)
        aggregate(0)
        stat(0, 1)
        deviation(0)
        coeff_a(1)
        turn_y(1, 1)
        mean_gamma(0)
        copy_y(1, 1, "dve")
        turn_y(1, 0)
        copy_y(1, 0, "act")
        coeff_b(0)
        turn_y(1, 2)
        copy_y(1, 2, "act")
        coeff_a(0)
        norm(1, 0, "dve")
        turn_y(1, 3)
        copy_y(1, 3, "act")
        norm(0, 0, "dve")
        turn_y(0, 1)
        copy_y(0, 1, "act")
        norm(1, 1, "dve")
        norm(0, 1, "dve")
        turn_y(0, 3)
        copy_y(0, 3, "act")
        turn_y(0, 2)
        copy_y(0, 2, "dve")
        turn_y(0, 0)
        copy_y(0, 0, "dve")
